import numpy as np
import ml_dtypes


def mxq(x, axis, fmt="e4m3"):
    dtype, down = {"e4m3": (ml_dtypes.float8_e4m3fn, 7), "e5m2": (ml_dtypes.float8_e5m2, 14)}[fmt]
    v = np.moveaxis(np.asarray(x, np.float32).astype(ml_dtypes.bfloat16).astype(np.float64), axis, -1)
    blocks = v.reshape(v.shape[:-1] + (-1, 32))
    amax = np.abs(blocks).max(-1, keepdims=True)
    byte = np.maximum(np.where(amax > 0, np.frexp(amax)[1] - 1 + 127, 0) - down, 1)
    scale = np.exp2(byte - 127.0)
    codes = (blocks / scale).astype(np.float32).astype(dtype).astype(np.float64)
    return np.moveaxis((codes * scale).reshape(v.shape), -1, axis)


BF16 = ml_dtypes.bfloat16


def bf(x):
    return np.asarray(x, np.float32).astype(BF16)


def f64(x):
    return np.asarray(x).astype(np.float64)


N, B, T, C, R, O, NC, H, W = 7, 128, 4, 256, 4, 8192, 128, 16, 4
BN_EPS = 1e-5
L2_EPS = 1e-12


def setup_inputs():
    off = 1.5 * np.random.standard_normal((N, 1, O))
    sd = 0.3 + 0.6 * np.random.random_sample((N, 1, O))
    col = (0.5 + np.random.random_sample((N, 1, NC))) / np.sqrt(O)
    return {"emb": bf(off + sd * np.random.standard_normal((N, B, O))),
            "gamma": bf(1.0 + 0.1 * np.random.standard_normal((N, O))),
            "beta": bf(0.1 * np.random.standard_normal((N, O))),
            "fc1d": bf(col * np.random.standard_normal((N, O, NC)))}


def reference(emb, gamma, beta, fc1d):
    e = f64(emb)
    mean = e.mean(axis=1, keepdims=True)
    var = ((e - mean) ** 2).mean(axis=1, keepdims=True)
    bn = f64(gamma)[:, None, :] * (e - mean) / np.sqrt(var + BN_EPS) + f64(beta)[:, None, :]
    bnn = bn / np.maximum(np.sqrt((bn ** 2).sum(axis=-1, keepdims=True)), L2_EPS)
    fc = f64(fc1d)
    fcn = fc / np.maximum(np.sqrt((fc ** 2).sum(axis=1, keepdims=True)), L2_EPS)
    logits = mxq(bnn, 2, "e4m3") @ mxq(fcn, 1, "e4m3")
    return np.transpose(logits, (1, 0, 2))

@@ -1,0 +1,227 @@
+from contextlib import ExitStack
+
+import concourse.mybir as mybir
+from concourse.masks import make_identity
+
+F32 = mybir.dt.float32
+BF16 = mybir.dt.bfloat16
+I32 = mybir.dt.int32
+U32 = mybir.dt.uint32
+U8 = mybir.dt.uint8
+FP8X4 = mybir.dt.float8_e4m3fn_x4
+ACT = mybir.ActivationFunctionType
+ALU = mybir.AluOpType
+
+P = 128
+BINS = 7
+FEATURES = 8192
+PACK = 4
+PASSES = FEATURES // (P * PACK)
+PAIRS = FEATURES // (2 * P)
+CHUNKS = FEATURES // P
+GROUPS = 8
+PAIRS_IN_GROUP = PAIRS // GROUPS
+CHUNKS_IN_GROUP = CHUNKS // GROUPS
+PIECES = 4
+PASSES_IN_PIECE = PASSES // PIECES
+BN_EPS = 1e-5
+L2_EPS = 1e-12
+
+FLOPS = 2 * BINS * P * FEATURES * P
+
+
+def tile_gmpahead_pb_k_kernel(tc, emb, gamma, beta, fc1d, out):
+    nc = tc.nc
+    with ExitStack() as stack:
+        const = stack.enter_context(tc.tile_pool(name="const", bufs=1))
+        emb_pool = stack.enter_context(tc.tile_pool(name="emb", bufs=2))
+        fc_pool = stack.enter_context(tc.tile_pool(name="fc", bufs=3))
+        bn_pool = stack.enter_context(tc.tile_pool(name="bn", bufs=2))
+        small = stack.enter_context(tc.tile_pool(name="small", bufs=2))
+        grouped = stack.enter_context(tc.tile_pool(name="grouped", bufs=2))
+        packed = stack.enter_context(tc.tile_pool(name="packed", bufs=2))
+        unused = stack.enter_context(tc.tile_pool(name="unused", bufs=2))
+        psum_emb = stack.enter_context(tc.psum_pool(name="psum_emb", bufs=2))
+        psum_bn = stack.enter_context(tc.psum_pool(name="psum_bn", bufs=2))
+        psum_fc = stack.enter_context(tc.psum_pool(name="psum_fc", bufs=2))
+        psum_one = stack.enter_context(tc.psum_pool(name="psum_one", bufs=1))
+
+        ident_f32 = const.tile([P, P], F32)
+        make_identity(nc, ident_f32[:])
+        ident_bf16 = const.tile([P, P], BF16)
+        make_identity(nc, ident_bf16[:])
+        bn_eps = const.tile([P, 1], F32)
+        nc.vector.memset(bn_eps[:], BN_EPS)
+        logits = const.tile([P, BINS, P], F32)
+
+        affine_rows = const.tile([P, BINS, 2 * P], BF16)
+        nc.vector.memset(affine_rows[64:128, :, :].bitcast(I32), 0)
+        nc.sync.dma_start(out=affine_rows[0:32, :, :], in_=gamma.rearrange("n (c x) -> c n x", x=2 * P))
+        nc.sync.dma_start(out=affine_rows[32:64, :, :], in_=beta.rearrange("n (c x) -> c n x", x=2 * P))
+        affine = const.tile([P, BINS, 2 * PAIRS, 2], F32)
+        for first in range(0, BINS, PAIRS_IN_GROUP):
+            count = min(PAIRS_IN_GROUP, BINS - first)
+            flipped = psum_emb.tile([P, PAIRS_IN_GROUP, P], F32, tag="emb_t")
+            for s in range(count):
+                nc.tensor.transpose(flipped[:, s, :], affine_rows[:, first + s, :].bitcast(F32), ident_f32[:])
+            pairs = flipped[:].bitcast(BF16).rearrange("p s (r e) -> p s r e", e=2)
+            nc.vector.tensor_copy(
+                out=affine[:, first : first + count, :, :], in_=pairs[:, 0:count, 0 : 2 * PAIRS, :]
+            )
+
+        state = {}
+
+        def load(n):
+            emb_rows = emb_pool.tile([P, FEATURES], BF16, tag="emb_rows")
+            nc.sync.dma_start(out=emb_rows[:], in_=emb[n])
+            fc_rows = fc_pool.tile([P, PASSES, PACK, P], BF16, tag="fc_rows")
+            nc.sync.dma_start(
+                out=fc_rows[:].rearrange("p g (u e) k -> p (g u) (e k)", e=2),
+                in_=fc1d[n].rearrange("(c p e) k -> p c (e k)", p=P, e=2),
+            )
+            state[n] = {
+                "emb_rows": emb_rows,
+                "fc_rows": fc_rows,
+                "bn_t": bn_pool.tile([P, PASSES, PACK, P], F32, tag="bn_t", name="bn_t"),
+                "stats": small.tile([P, PAIRS, 6], F32, tag="stats", name="stats"),
+                "spread": small.tile([P, PAIRS, 2], F32, tag="spread", name="spread"),
+                "gain": small.tile([P, PAIRS, 2], F32, tag="gain", name="gain"),
+                "shift": small.tile([P, PAIRS, 2], F32, tag="shift", name="shift"),
+                "bn_squares": small.tile([P, 2 * GROUPS], F32, tag="bn_squares", name="bn_squares"),
+                "fc_squares": small.tile([P, GROUPS], F32, tag="fc_squares", name="fc_squares"),
+            }
+
+        def batch_norm_group(n, i):
+            s_n = state[n]
+            words = s_n["emb_rows"][:].bitcast(F32)
+            emb_t = psum_emb.tile([P, PAIRS_IN_GROUP, P], F32, tag="emb_t")
+            for s in range(PAIRS_IN_GROUP):
+                c = PAIRS_IN_GROUP * i + s
+                nc.tensor.transpose(emb_t[:, s, :], words[:, P * c : P * (c + 1)], ident_f32[:])
+            both = emb_t[:].bitcast(BF16)
+            chunks = slice(PAIRS_IN_GROUP * i, PAIRS_IN_GROUP * (i + 1))
+            for s in range(PAIRS_IN_GROUP):
+                nc.vector.bn_stats(out=s_n["stats"][:, PAIRS_IN_GROUP * i + s, :], in_=both[:, s, :])
+            moments = s_n["stats"][:, chunks, :].rearrange("p c (e m) -> p c e m", m=3)
+            mean = moments[:, :, :, 1]
+            sum_sq_dev = moments[:, :, :, 2]
+            spread = s_n["spread"][:, chunks, :]
+            gain = s_n["gain"][:, chunks, :]
+            shift = s_n["shift"][:, chunks, :]
+            nc.scalar.activation(out=spread, in_=sum_sq_dev, func=ACT.Sqrt, bias=bn_eps[:], scale=1.0 / P)
+            nc.vector.reciprocal(out=spread, in_=spread)
+            nc.vector.tensor_tensor(out=gain, in0=spread, in1=affine[:, n, chunks, :], op=ALU.mult)
+            nc.vector.tensor_tensor(out=shift, in0=gain, in1=mean, op=ALU.mult)
+            nc.vector.tensor_tensor(
+                out=shift,
+                in0=affine[:, n, PAIRS + PAIRS_IN_GROUP * i : PAIRS + PAIRS_IN_GROUP * (i + 1), :],
+                in1=shift,
+                op=ALU.subtract,
+            )
+            split = both.rearrange("p s (b e) -> p s b e", e=2)
+            bn_chunks = s_n["bn_t"][:].rearrange("p g (u e) b -> p (g u) e b", e=2)
+            for s in range(PAIRS_IN_GROUP):
+                c = PAIRS_IN_GROUP * i + s
+                for e in range(2):
+                    nc.scalar.activation(
+                        out=bn_chunks[:, c, e, :],
+                        in_=split[:, s, :, e],
+                        func=ACT.Identity,
+                        bias=s_n["shift"][:, c, e : e + 1],
+                        scale=s_n["gain"][:, c, e : e + 1],
+                    )
+            for half in range(2):
+                bn_rows = psum_bn.tile([P, PAIRS_IN_GROUP, P], F32, tag="bn_rows")
+                for s in range(PAIRS_IN_GROUP):
+                    c = PAIRS_IN_GROUP * i + 2 * half + s // 2
+                    nc.tensor.transpose(bn_rows[:, s, :], bn_chunks[:, c, s % 2, :], ident_f32[:])
+                squares = unused.tile([P, PAIRS_IN_GROUP, P], BF16, tag="squares")
+                nc.scalar.activation(
+                    out=squares[:],
+                    in_=bn_rows[:],
+                    func=ACT.Square,
+                    accum_out=s_n["bn_squares"][:, 2 * i + half : 2 * i + half + 1],
+                )
+
+        def fc_squares_group(n, i):
+            s_n = state[n]
+            fc_chunks = s_n["fc_rows"][:].rearrange("p g t k -> p (g t) k")
+            fc_t = psum_fc.tile([P, CHUNKS_IN_GROUP, P], BF16, tag="fc_t")
+            for s in range(CHUNKS_IN_GROUP):
+                nc.tensor.transpose(fc_t[:, s, :], fc_chunks[:, CHUNKS_IN_GROUP * i + s, :], ident_bf16[:])
+            squares = unused.tile([P, CHUNKS_IN_GROUP, P], BF16, tag="fc_sq")
+            nc.scalar.activation(
+                out=squares[:], in_=fc_t[:], func=ACT.Square, accum_out=s_n["fc_squares"][:, i : i + 1]
+            )
+
+        def inverse_norms(n):
+            s_n = state[n]
+            spread_out = psum_one.tile([P, 2, P], F32, tag="spread_out")
+            for which, name in enumerate(("bn_squares", "fc_squares")):
+                norm = small.tile([P, 1], F32, tag="norm" + name)
+                nc.vector.reduce_sum(out=norm[:], in_=s_n[name][:], axis=mybir.AxisListType.X)
+                nc.vector.tensor_scalar_max(out=norm[:], in0=norm[:], scalar1=L2_EPS * L2_EPS)
+                nc.scalar.activation(out=norm[:], in_=norm[:], func=ACT.Sqrt)
+                nc.vector.reciprocal(out=norm[:], in_=norm[:])
+                nc.tensor.matmul(
+                    spread_out[:, which, :],
+                    lhsT=norm[:, 0:1].to_broadcast([P, P]),
+                    rhs=ident_f32[:],
+                    start=True,
+                    stop=True,
+                )
+            s_n["inverse"] = spread_out
+            s_n["codes"] = {}
+            s_n["scales"] = {}
+            for name in ("bn", "fc"):
+                s_n["codes"][name] = packed.tile([P, PASSES * P], U32, tag="codes" + name, name="codes", align_bytes=64)
+                s_n["scales"][name] = packed.tile([P, PASSES * P], U8, tag="scales" + name, name="scales", align_bytes=64)
+            s_n["acc"] = psum_one.tile([P, P], F32, tag="acc", name="acc")
+
+        def quantise_and_multiply(n, j):
+            s_n = state[n]
+            passes = slice(PASSES_IN_PIECE * j, PASSES_IN_PIECE * (j + 1))
+            cols = slice(PASSES_IN_PIECE * P * j, PASSES_IN_PIECE * P * (j + 1))
+            for which, name, source in ((0, "bn", s_n["bn_t"]), (1, "fc", s_n["fc_rows"])):
+                side_by_side = grouped.tile([P, PASSES_IN_PIECE, P, PACK], BF16, tag="g" + name, align_bytes=64)
+                nc.vector.tensor_tensor(
+                    out=side_by_side[:],
+                    in0=source[:, passes, :, :].rearrange("p g t c -> p g c t"),
+                    in1=s_n["inverse"][:, which, :].unsqueeze(1).unsqueeze(3).to_broadcast([P, PASSES_IN_PIECE, P, PACK]),
+                    op=ALU.mult,
+                )
+                nc.vector.quantize_mx(
+                    out=s_n["codes"][name][:, cols].bitcast(FP8X4),
+                    scales=s_n["scales"][name][:, cols],
+                    in_=side_by_side[:].rearrange("p g c t -> p (g c t)"),
+                )
+            for g in range(PASSES_IN_PIECE * j, PASSES_IN_PIECE * (j + 1)):
+                one = slice(P * g, P * (g + 1))
+                nc.tensor.matmul_mx(
+                    out=s_n["acc"][:],
+                    lhsT=s_n["codes"]["bn"][:, one].bitcast(FP8X4),
+                    lhsT_scale=s_n["scales"]["bn"][:, one],
+                    rhs=s_n["codes"]["fc"][:, one].bitcast(FP8X4),
+                    rhs_scale=s_n["scales"]["fc"][:, one],
+                    start=(g == 0),
+                    stop=(g == PASSES - 1),
+                )
+
+        def store(n):
+            nc.scalar.copy(out=logits[:, n, :], in_=state[n]["acc"][:])
+            nc.sync.dma_start(out=out[:, n, :], in_=logits[:, n, :])
+
+        load(0)
+        for n in range(BINS + 1):
+            if n + 1 < BINS:
+                load(n + 1)
+            for i in range(GROUPS):
+                if n < BINS:
+                    batch_norm_group(n, i)
+                    fc_squares_group(n, i)
+                if n > 0 and i % 2 == 1:
+                    quantise_and_multiply(n - 1, i // 2)
+            if n > 0:
+                store(n - 1)
+            if n < BINS:
+                inverse_norms(n)

@@ -24,6 +24,8 @@ PAIRS_IN_GROUP = PAIRS // GROUPS
 CHUNKS_IN_GROUP = CHUNKS // GROUPS
 PIECES = 4
 PASSES_IN_PIECE = PASSES // PIECES
+SLOTS = BINS * GROUPS
+FC_AHEAD = GROUPS + 1
 BN_EPS = 1e-5
 L2_EPS = 1e-12
 
@@ -54,10 +56,41 @@ def tile_gmpahead_pb_k_kernel(tc, emb, gamma, beta, fc1d, out):
         nc.vector.memset(bn_eps[:], BN_EPS)
         logits = const.tile([P, BINS, P], F32)
 
+        emb_rows = {}
+        fc_rows = {}
+        bn_t = {}
+        per_bin = {}
+        emb_t = {}
+        fc_t = {}
+        inverse = {}
+        side_by_side = {}
+        codes = {}
+        scales = {}
+        acc = {}
+
+        def load_emb(n):
+            emb_rows[n] = emb_pool.tile([P, FEATURES], BF16, tag="emb_rows", name="emb_rows")
+            quarter = FEATURES // 4
+            for q in range(4):
+                cols = slice(quarter * q, quarter * (q + 1))
+                nc.sync.dma_start(out=emb_rows[n][:, cols], in_=emb[n][:, cols])
+
+        def load_fc(n):
+            fc_rows[n] = fc_pool.tile([P, PASSES, PACK, P], BF16, tag="fc_rows", name="fc_rows")
+            into = fc_rows[n][:].rearrange("p g (u e) k -> p (g u) (e k)", e=2)
+            source = fc1d[n].rearrange("(c p e) k -> p c (e k)", p=P, e=2)
+            quarter = PAIRS // 4
+            for q in range(4):
+                some = slice(quarter * q, quarter * (q + 1))
+                nc.sync.dma_start(out=into[:, some, :], in_=source[:, some, :])
+
+        load_fc(0)
+        load_emb(0)
+
         affine_rows = const.tile([P, BINS, 2 * P], BF16)
         nc.vector.memset(affine_rows[64:128, :, :].bitcast(I32), 0)
-        nc.sync.dma_start(out=affine_rows[0:32, :, :], in_=gamma.rearrange("n (c x) -> c n x", x=2 * P))
-        nc.sync.dma_start(out=affine_rows[32:64, :, :], in_=beta.rearrange("n (c x) -> c n x", x=2 * P))
+        nc.scalar.dma_start(out=affine_rows[0:32, :, :], in_=gamma.rearrange("n (c x) -> c n x", x=2 * P))
+        nc.scalar.dma_start(out=affine_rows[32:64, :, :], in_=beta.rearrange("n (c x) -> c n x", x=2 * P))
         affine = const.tile([P, BINS, 2 * PAIRS, 2], F32)
         for first in range(0, BINS, PAIRS_IN_GROUP):
             count = min(PAIRS_IN_GROUP, BINS - first)
@@ -69,159 +102,212 @@ def tile_gmpahead_pb_k_kernel(tc, emb, gamma, beta, fc1d, out):
                 out=affine[:, first : first + count, :, :], in_=pairs[:, 0:count, 0 : 2 * PAIRS, :]
             )
 
-        state = {}
+        load_fc(1)
+        load_emb(1)
+        load_fc(2)
 
-        def load(n):
-            emb_rows = emb_pool.tile([P, FEATURES], BF16, tag="emb_rows")
-            nc.sync.dma_start(out=emb_rows[:], in_=emb[n])
-            fc_rows = fc_pool.tile([P, PASSES, PACK, P], BF16, tag="fc_rows")
-            nc.sync.dma_start(
-                out=fc_rows[:].rearrange("p g (u e) k -> p (g u) (e k)", e=2),
-                in_=fc1d[n].rearrange("(c p e) k -> p c (e k)", p=P, e=2),
-            )
-            state[n] = {
-                "emb_rows": emb_rows,
-                "fc_rows": fc_rows,
-                "bn_t": bn_pool.tile([P, PASSES, PACK, P], F32, tag="bn_t", name="bn_t"),
+        def open_bin(n):
+            bn_t[n] = bn_pool.tile([P, PASSES, PACK, P], F32, tag="bn_t", name="bn_t")
+            per_bin[n] = {
                 "stats": small.tile([P, PAIRS, 6], F32, tag="stats", name="stats"),
                 "spread": small.tile([P, PAIRS, 2], F32, tag="spread", name="spread"),
                 "gain": small.tile([P, PAIRS, 2], F32, tag="gain", name="gain"),
                 "shift": small.tile([P, PAIRS, 2], F32, tag="shift", name="shift"),
                 "bn_squares": small.tile([P, 2 * GROUPS], F32, tag="bn_squares", name="bn_squares"),
-                "fc_squares": small.tile([P, GROUPS], F32, tag="fc_squares", name="fc_squares"),
             }
 
-        def batch_norm_group(n, i):
-            s_n = state[n]
-            words = s_n["emb_rows"][:].bitcast(F32)
-            emb_t = psum_emb.tile([P, PAIRS_IN_GROUP, P], F32, tag="emb_t")
+        def transpose_emb(slot):
+            n, i = divmod(slot, GROUPS)
+            words = emb_rows[n][:].bitcast(F32)
+            emb_t[slot] = psum_emb.tile([P, PAIRS_IN_GROUP, P], F32, tag="emb_t", name="emb_t")
             for s in range(PAIRS_IN_GROUP):
                 c = PAIRS_IN_GROUP * i + s
-                nc.tensor.transpose(emb_t[:, s, :], words[:, P * c : P * (c + 1)], ident_f32[:])
-            both = emb_t[:].bitcast(BF16)
-            chunks = slice(PAIRS_IN_GROUP * i, PAIRS_IN_GROUP * (i + 1))
+                nc.tensor.transpose(emb_t[slot][:, s, :], words[:, P * c : P * (c + 1)], ident_f32[:])
+
+        def statistics(slot):
+            n, i = divmod(slot, GROUPS)
+            both = emb_t[slot][:].bitcast(BF16)
             for s in range(PAIRS_IN_GROUP):
-                nc.vector.bn_stats(out=s_n["stats"][:, PAIRS_IN_GROUP * i + s, :], in_=both[:, s, :])
-            moments = s_n["stats"][:, chunks, :].rearrange("p c (e m) -> p c e m", m=3)
-            mean = moments[:, :, :, 1]
-            sum_sq_dev = moments[:, :, :, 2]
-            spread = s_n["spread"][:, chunks, :]
-            gain = s_n["gain"][:, chunks, :]
-            shift = s_n["shift"][:, chunks, :]
-            nc.scalar.activation(out=spread, in_=sum_sq_dev, func=ACT.Sqrt, bias=bn_eps[:], scale=1.0 / P)
+                nc.vector.bn_stats(out=per_bin[n]["stats"][:, PAIRS_IN_GROUP * i + s, :], in_=both[:, s, :])
+            chunks = slice(PAIRS_IN_GROUP * i, PAIRS_IN_GROUP * (i + 1))
+            moments = per_bin[n]["stats"][:, chunks, :].rearrange("p c (e m) -> p c e m", m=3)
+            nc.scalar.activation(
+                out=per_bin[n]["spread"][:, chunks, :],
+                in_=moments[:, :, :, 2],
+                func=ACT.Sqrt,
+                bias=bn_eps[:],
+                scale=1.0 / P,
+            )
+
+        def gain_and_shift(slot):
+            n, i = divmod(slot, GROUPS)
+            chunks = slice(PAIRS_IN_GROUP * i, PAIRS_IN_GROUP * (i + 1))
+            beta_chunks = slice(PAIRS + PAIRS_IN_GROUP * i, PAIRS + PAIRS_IN_GROUP * (i + 1))
+            moments = per_bin[n]["stats"][:, chunks, :].rearrange("p c (e m) -> p c e m", m=3)
+            spread = per_bin[n]["spread"][:, chunks, :]
+            gain = per_bin[n]["gain"][:, chunks, :]
+            shift = per_bin[n]["shift"][:, chunks, :]
             nc.vector.reciprocal(out=spread, in_=spread)
             nc.vector.tensor_tensor(out=gain, in0=spread, in1=affine[:, n, chunks, :], op=ALU.mult)
-            nc.vector.tensor_tensor(out=shift, in0=gain, in1=mean, op=ALU.mult)
-            nc.vector.tensor_tensor(
-                out=shift,
-                in0=affine[:, n, PAIRS + PAIRS_IN_GROUP * i : PAIRS + PAIRS_IN_GROUP * (i + 1), :],
-                in1=shift,
-                op=ALU.subtract,
-            )
-            split = both.rearrange("p s (b e) -> p s b e", e=2)
-            bn_chunks = s_n["bn_t"][:].rearrange("p g (u e) b -> p (g u) e b", e=2)
-            for s in range(PAIRS_IN_GROUP):
-                c = PAIRS_IN_GROUP * i + s
-                for e in range(2):
-                    nc.scalar.activation(
-                        out=bn_chunks[:, c, e, :],
-                        in_=split[:, s, :, e],
-                        func=ACT.Identity,
-                        bias=s_n["shift"][:, c, e : e + 1],
-                        scale=s_n["gain"][:, c, e : e + 1],
-                    )
+            nc.vector.tensor_tensor(out=shift, in0=gain, in1=moments[:, :, :, 1], op=ALU.mult)
+            nc.vector.tensor_tensor(out=shift, in0=affine[:, n, beta_chunks, :], in1=shift, op=ALU.subtract)
+
+        def batch_norm(slot):
+            n, i = divmod(slot, GROUPS)
+            split = emb_t[slot][:].bitcast(BF16).rearrange("p s (b e) -> p s b e", e=2)
+            bn_chunks = bn_t[n][:].rearrange("p g (u e) b -> p (g u) e b", e=2)
+            bn_rows = {}
             for half in range(2):
-                bn_rows = psum_bn.tile([P, PAIRS_IN_GROUP, P], F32, tag="bn_rows")
+                bn_rows[half] = psum_bn.tile([P, PAIRS_IN_GROUP, P], F32, tag="bn_rows", name="bn_rows")
                 for s in range(PAIRS_IN_GROUP):
                     c = PAIRS_IN_GROUP * i + 2 * half + s // 2
-                    nc.tensor.transpose(bn_rows[:, s, :], bn_chunks[:, c, s % 2, :], ident_f32[:])
+                    e = s % 2
+                    nc.scalar.activation(
+                        out=bn_chunks[:, c, e, :],
+                        in_=split[:, 2 * half + s // 2, :, e],
+                        func=ACT.Identity,
+                        bias=per_bin[n]["shift"][:, c, e : e + 1],
+                        scale=per_bin[n]["gain"][:, c, e : e + 1],
+                    )
+                    nc.tensor.transpose(bn_rows[half][:, s, :], bn_chunks[:, c, e, :], ident_f32[:])
+            return bn_rows
+
+        def bn_squares(slot, bn_rows):
+            n, i = divmod(slot, GROUPS)
+            for half in range(2):
                 squares = unused.tile([P, PAIRS_IN_GROUP, P], BF16, tag="squares")
                 nc.scalar.activation(
                     out=squares[:],
-                    in_=bn_rows[:],
+                    in_=bn_rows[half][:],
                     func=ACT.Square,
-                    accum_out=s_n["bn_squares"][:, 2 * i + half : 2 * i + half + 1],
+                    accum_out=per_bin[n]["bn_squares"][:, 2 * i + half : 2 * i + half + 1],
                 )
 
-        def fc_squares_group(n, i):
-            s_n = state[n]
-            fc_chunks = s_n["fc_rows"][:].rearrange("p g t k -> p (g t) k")
-            fc_t = psum_fc.tile([P, CHUNKS_IN_GROUP, P], BF16, tag="fc_t")
+        def transpose_fc(slot):
+            n, i = divmod(slot, GROUPS)
+            fc_chunks = fc_rows[n][:].rearrange("p g t k -> p (g t) k")
+            fc_t[slot] = psum_fc.tile([P, CHUNKS_IN_GROUP, P], BF16, tag="fc_t", name="fc_t")
             for s in range(CHUNKS_IN_GROUP):
-                nc.tensor.transpose(fc_t[:, s, :], fc_chunks[:, CHUNKS_IN_GROUP * i + s, :], ident_bf16[:])
+                nc.tensor.transpose(fc_t[slot][:, s, :], fc_chunks[:, CHUNKS_IN_GROUP * i + s, :], ident_bf16[:])
+
+        def fc_squares(slot):
+            n, i = divmod(slot, GROUPS)
+            if i == 0:
+                per_bin[("fc", n)] = small.tile([P, GROUPS], F32, tag="fc_squares", name="fc_squares")
             squares = unused.tile([P, CHUNKS_IN_GROUP, P], BF16, tag="fc_sq")
             nc.scalar.activation(
-                out=squares[:], in_=fc_t[:], func=ACT.Square, accum_out=s_n["fc_squares"][:, i : i + 1]
+                out=squares[:], in_=fc_t[slot][:], func=ACT.Square, accum_out=per_bin[("fc", n)][:, i : i + 1]
             )
 
-        def inverse_norms(n):
-            s_n = state[n]
-            spread_out = psum_one.tile([P, 2, P], F32, tag="spread_out")
-            for which, name in enumerate(("bn_squares", "fc_squares")):
-                norm = small.tile([P, 1], F32, tag="norm" + name)
-                nc.vector.reduce_sum(out=norm[:], in_=s_n[name][:], axis=mybir.AxisListType.X)
-                nc.vector.tensor_scalar_max(out=norm[:], in0=norm[:], scalar1=L2_EPS * L2_EPS)
-                nc.scalar.activation(out=norm[:], in_=norm[:], func=ACT.Sqrt)
-                nc.vector.reciprocal(out=norm[:], in_=norm[:])
-                nc.tensor.matmul(
-                    spread_out[:, which, :],
-                    lhsT=norm[:, 0:1].to_broadcast([P, P]),
-                    rhs=ident_f32[:],
-                    start=True,
-                    stop=True,
-                )
-            s_n["inverse"] = spread_out
-            s_n["codes"] = {}
-            s_n["scales"] = {}
-            for name in ("bn", "fc"):
-                s_n["codes"][name] = packed.tile([P, PASSES * P], U32, tag="codes" + name, name="codes", align_bytes=64)
-                s_n["scales"][name] = packed.tile([P, PASSES * P], U8, tag="scales" + name, name="scales", align_bytes=64)
-            s_n["acc"] = psum_one.tile([P, P], F32, tag="acc", name="acc")
+        def norm_root(sums, name):
+            norm = small.tile([P, 1], F32, tag="norm" + name, name="norm")
+            nc.vector.reduce_sum(out=norm[:], in_=sums[:], axis=mybir.AxisListType.X)
+            nc.vector.tensor_scalar_max(out=norm[:], in0=norm[:], scalar1=L2_EPS * L2_EPS)
+            nc.scalar.activation(out=norm[:], in_=norm[:], func=ACT.Sqrt)
+            return norm
 
-        def quantise_and_multiply(n, j):
-            s_n = state[n]
+        def spread_inverse(norm, into):
+            nc.vector.reciprocal(out=norm[:], in_=norm[:])
+            nc.tensor.matmul(into, lhsT=norm[:, 0:1].to_broadcast([P, P]), rhs=ident_f32[:], start=True, stop=True)
+
+        def scale(engine, name, source, n, j):
             passes = slice(PASSES_IN_PIECE * j, PASSES_IN_PIECE * (j + 1))
+            result = grouped.tile([P, PASSES_IN_PIECE, P, PACK], BF16, tag="g" + name, name="g", align_bytes=64)
+            engine.tensor_tensor(
+                out=result[:],
+                in0=source[:, passes, :, :].rearrange("p g t c -> p g c t"),
+                in1=inverse[(name, n)].unsqueeze(1).unsqueeze(3).to_broadcast([P, PASSES_IN_PIECE, P, PACK]),
+                op=ALU.mult,
+            )
+            side_by_side[(name, n, j)] = result
+
+        def quantise(name, n, j):
+            if j == 0:
+                codes[(name, n)] = packed.tile([P, PASSES * P], U32, tag="c" + name, name="c", align_bytes=64)
+                scales[(name, n)] = packed.tile([P, PASSES * P], U8, tag="s" + name, name="s", align_bytes=64)
             cols = slice(PASSES_IN_PIECE * P * j, PASSES_IN_PIECE * P * (j + 1))
-            for which, name, source in ((0, "bn", s_n["bn_t"]), (1, "fc", s_n["fc_rows"])):
-                side_by_side = grouped.tile([P, PASSES_IN_PIECE, P, PACK], BF16, tag="g" + name, align_bytes=64)
-                nc.vector.tensor_tensor(
-                    out=side_by_side[:],
-                    in0=source[:, passes, :, :].rearrange("p g t c -> p g c t"),
-                    in1=s_n["inverse"][:, which, :].unsqueeze(1).unsqueeze(3).to_broadcast([P, PASSES_IN_PIECE, P, PACK]),
-                    op=ALU.mult,
-                )
-                nc.vector.quantize_mx(
-                    out=s_n["codes"][name][:, cols].bitcast(FP8X4),
-                    scales=s_n["scales"][name][:, cols],
-                    in_=side_by_side[:].rearrange("p g c t -> p (g c t)"),
-                )
+            nc.vector.quantize_mx(
+                out=codes[(name, n)][:, cols].bitcast(FP8X4),
+                scales=scales[(name, n)][:, cols],
+                in_=side_by_side[(name, n, j)][:].rearrange("p g c t -> p (g c t)"),
+            )
+
+        def multiply(n, j):
+            if j == 0:
+                acc[n] = psum_one.tile([P, P], F32, tag="acc", name="acc")
             for g in range(PASSES_IN_PIECE * j, PASSES_IN_PIECE * (j + 1)):
                 one = slice(P * g, P * (g + 1))
                 nc.tensor.matmul_mx(
-                    out=s_n["acc"][:],
-                    lhsT=s_n["codes"]["bn"][:, one].bitcast(FP8X4),
-                    lhsT_scale=s_n["scales"]["bn"][:, one],
-                    rhs=s_n["codes"]["fc"][:, one].bitcast(FP8X4),
-                    rhs_scale=s_n["scales"]["fc"][:, one],
+                    out=acc[n][:],
+                    lhsT=codes[("bn", n)][:, one].bitcast(FP8X4),
+                    lhsT_scale=scales[("bn", n)][:, one],
+                    rhs=codes[("fc", n)][:, one].bitcast(FP8X4),
+                    rhs_scale=scales[("fc", n)][:, one],
                     start=(g == 0),
                     stop=(g == PASSES - 1),
                 )
+            if j == PIECES - 1:
+                nc.scalar.copy(out=logits[:, n, :], in_=acc[n][:])
+                nc.sync.dma_start(out=out[:, n, :], in_=logits[:, n, :])
 
-        def store(n):
-            nc.scalar.copy(out=logits[:, n, :], in_=state[n]["acc"][:])
-            nc.sync.dma_start(out=out[:, n, :], in_=logits[:, n, :])
+        def is_slot(slot):
+            return 0 <= slot < SLOTS
 
-        load(0)
-        for n in range(BINS + 1):
-            if n + 1 < BINS:
-                load(n + 1)
-            for i in range(GROUPS):
-                if n < BINS:
-                    batch_norm_group(n, i)
-                    fc_squares_group(n, i)
-                if n > 0 and i % 2 == 1:
-                    quantise_and_multiply(n - 1, i // 2)
-            if n > 0:
-                store(n - 1)
-            if n < BINS:
-                inverse_norms(n)
+        norms = {}
+        with tc.manual_schedule():
+            for r in range(-FC_AHEAD - 1, SLOTS + GROUPS + 2):
+                n, i = divmod(r, GROUPS)
+                if is_slot(r + 2) and (r + 2) % GROUPS == 0:
+                    open_bin((r + 2) // GROUPS)
+                if i == GROUPS - 2 and 0 <= n and n + 2 < BINS:
+                    load_emb(n + 2)
+                if i == 0 and 1 <= n and n + 2 < BINS:
+                    load_fc(n + 2)
+
+                if is_slot(r):
+                    bn_rows = batch_norm(r)
+                if is_slot(r + 2):
+                    transpose_emb(r + 2)
+                if is_slot(r + 1):
+                    statistics(r + 1)
+                if is_slot(r):
+                    bn_squares(r, bn_rows)
+                if is_slot(r + FC_AHEAD):
+                    fc_squares(r + FC_AHEAD)
+                if is_slot(r + FC_AHEAD + 1):
+                    transpose_fc(r + FC_AHEAD + 1)
+
+                if i == 0 and 1 <= n <= BINS:
+                    norms["bn"] = norm_root(per_bin[n - 1]["bn_squares"], "bn")
+                if i == GROUPS - 1 and 0 <= n + 1 < BINS:
+                    norms["fc"] = norm_root(per_bin[("fc", n + 1)], "fc")
+
+                if i % 2 == 0 and 1 <= n <= BINS and i > 0:
+                    quantise("bn", n - 1, i // 2 - 1)
+                if i == 0 and 2 <= n <= BINS + 1:
+                    quantise("bn", n - 2, PIECES - 1)
+                if i % 2 == 1 and 0 <= n < BINS:
+                    quantise("fc", n, i // 2)
+                if i % 2 == 1 and 1 <= n <= BINS:
+                    scale(nc.vector, "bn", bn_t[n - 1], n - 1, i // 2)
+                if i % 2 == 0 and 0 <= n < BINS:
+                    scale(nc.vector, "fc", fc_rows[n], n, i // 2)
+
+                if i == 0 and 1 <= n <= BINS:
+                    inverse_bn = psum_one.tile([P, P], F32, tag="inverse_bn")
+                    spread_inverse(norms["bn"], inverse_bn[:])
+                    inverse[("bn", n - 1)] = inverse_bn[:]
+                if i == GROUPS - 1 and 0 <= n + 1 < BINS:
+                    inverse_ps = psum_bn.tile([P, PAIRS_IN_GROUP, P], F32, tag="bn_rows")
+                    spread_inverse(norms["fc"], inverse_ps[:, 0, :])
+                    inverse_fc = small.tile([P, P], F32, tag="inverse_fc")
+                    nc.scalar.copy(out=inverse_fc[:], in_=inverse_ps[:, 0, :])
+                    inverse[("fc", n + 1)] = inverse_fc[:]
+
+                if is_slot(r + 1):
+                    gain_and_shift(r + 1)
+
+                if i % 2 == 0 and 1 <= n <= BINS and i > 0:
+                    multiply(n - 1, i // 2 - 1)
+                if i == 0 and 2 <= n <= BINS + 1:
+                    multiply(n - 2, PIECES - 1)

@@ -26,10 +26,23 @@ PIECES = 4
 PASSES_IN_PIECE = PASSES // PIECES
 SLOTS = BINS * GROUPS
 FC_AHEAD = GROUPS + 1
+VECTOR_CHUNKS = 2
 BN_EPS = 1e-5
 L2_EPS = 1e-12
 
 FLOPS = 2 * BINS * P * FEATURES * P
+
+
+def is_slot(k):
+    return 0 <= k < SLOTS
+
+
+def first_of_bin(k):
+    return k // GROUPS if is_slot(k) and k % GROUPS == 0 else None
+
+
+def piece_of_bin(k):
+    return (k // GROUPS, k % GROUPS // 2) if is_slot(k) and k % 2 == 0 else None
 
 
 def tile_gmpahead_pb_k_kernel(tc, emb, gamma, beta, fc1d, out):
@@ -43,9 +56,9 @@ def tile_gmpahead_pb_k_kernel(tc, emb, gamma, beta, fc1d, out):
         grouped = stack.enter_context(tc.tile_pool(name="grouped", bufs=2))
         packed = stack.enter_context(tc.tile_pool(name="packed", bufs=2))
         unused = stack.enter_context(tc.tile_pool(name="unused", bufs=2))
-        psum_emb = stack.enter_context(tc.psum_pool(name="psum_emb", bufs=2))
+        psum_emb = stack.enter_context(tc.psum_pool(name="psum_emb", bufs=3))
         psum_bn = stack.enter_context(tc.psum_pool(name="psum_bn", bufs=2))
-        psum_fc = stack.enter_context(tc.psum_pool(name="psum_fc", bufs=2))
+        psum_fc = stack.enter_context(tc.psum_pool(name="psum_fc", bufs=1))
         psum_one = stack.enter_context(tc.psum_pool(name="psum_one", bufs=1))
 
         ident_f32 = const.tile([P, P], F32)
@@ -60,8 +73,11 @@ def tile_gmpahead_pb_k_kernel(tc, emb, gamma, beta, fc1d, out):
         fc_rows = {}
         bn_t = {}
         per_bin = {}
+        squares_sum = {}
         emb_t = {}
+        bn_rows = {}
         fc_t = {}
+        norm = {}
         inverse = {}
         side_by_side = {}
         codes = {}
@@ -113,8 +129,8 @@ def tile_gmpahead_pb_k_kernel(tc, emb, gamma, beta, fc1d, out):
                 "spread": small.tile([P, PAIRS, 2], F32, tag="spread", name="spread"),
                 "gain": small.tile([P, PAIRS, 2], F32, tag="gain", name="gain"),
                 "shift": small.tile([P, PAIRS, 2], F32, tag="shift", name="shift"),
-                "bn_squares": small.tile([P, 2 * GROUPS], F32, tag="bn_squares", name="bn_squares"),
             }
+            squares_sum[("bn", n)] = small.tile([P, 2 * GROUPS], F32, tag="bn_squares", name="bn_squares")
 
         def transpose_emb(slot):
             n, i = divmod(slot, GROUPS)
@@ -129,6 +145,9 @@ def tile_gmpahead_pb_k_kernel(tc, emb, gamma, beta, fc1d, out):
             both = emb_t[slot][:].bitcast(BF16)
             for s in range(PAIRS_IN_GROUP):
                 nc.vector.bn_stats(out=per_bin[n]["stats"][:, PAIRS_IN_GROUP * i + s, :], in_=both[:, s, :])
+
+        def deviation(slot):
+            n, i = divmod(slot, GROUPS)
             chunks = slice(PAIRS_IN_GROUP * i, PAIRS_IN_GROUP * (i + 1))
             moments = per_bin[n]["stats"][:, chunks, :].rearrange("p c (e m) -> p c e m", m=3)
             nc.scalar.activation(
@@ -148,39 +167,42 @@ def tile_gmpahead_pb_k_kernel(tc, emb, gamma, beta, fc1d, out):
             gain = per_bin[n]["gain"][:, chunks, :]
             shift = per_bin[n]["shift"][:, chunks, :]
             nc.vector.reciprocal(out=spread, in_=spread)
-            nc.vector.tensor_tensor(out=gain, in0=spread, in1=affine[:, n, chunks, :], op=ALU.mult)
-            nc.vector.tensor_tensor(out=shift, in0=gain, in1=moments[:, :, :, 1], op=ALU.mult)
-            nc.vector.tensor_tensor(out=shift, in0=affine[:, n, beta_chunks, :], in1=shift, op=ALU.subtract)
+            nc.gpsimd.tensor_tensor(out=gain, in0=spread, in1=affine[:, n, chunks, :], op=ALU.mult)
+            nc.gpsimd.tensor_tensor(out=shift, in0=gain, in1=moments[:, :, :, 1], op=ALU.mult)
+            nc.gpsimd.tensor_tensor(out=shift, in0=affine[:, n, beta_chunks, :], in1=shift, op=ALU.subtract)
 
         def batch_norm(slot):
             n, i = divmod(slot, GROUPS)
             split = emb_t[slot][:].bitcast(BF16).rearrange("p s (b e) -> p s b e", e=2)
             bn_chunks = bn_t[n][:].rearrange("p g (u e) b -> p (g u) e b", e=2)
-            bn_rows = {}
-            for half in range(2):
-                bn_rows[half] = psum_bn.tile([P, PAIRS_IN_GROUP, P], F32, tag="bn_rows", name="bn_rows")
-                for s in range(PAIRS_IN_GROUP):
-                    c = PAIRS_IN_GROUP * i + 2 * half + s // 2
-                    e = s % 2
+            for q in range(CHUNKS_IN_GROUP):
+                half, place = divmod(q, PAIRS_IN_GROUP)
+                s, e = divmod(q, 2)
+                c = PAIRS_IN_GROUP * i + s
+                if place == 0:
+                    bn_rows[(slot, half)] = psum_bn.tile([P, PAIRS_IN_GROUP, P], F32, tag="bn_rows", name="bn_rows")
+                gain = per_bin[n]["gain"][:, c, e : e + 1]
+                shift = per_bin[n]["shift"][:, c, e : e + 1]
+                if q < CHUNKS_IN_GROUP - VECTOR_CHUNKS:
                     nc.scalar.activation(
-                        out=bn_chunks[:, c, e, :],
-                        in_=split[:, 2 * half + s // 2, :, e],
-                        func=ACT.Identity,
-                        bias=per_bin[n]["shift"][:, c, e : e + 1],
-                        scale=per_bin[n]["gain"][:, c, e : e + 1],
+                        out=bn_chunks[:, c, e, :], in_=split[:, s, :, e], func=ACT.Identity, bias=shift, scale=gain
                     )
-                    nc.tensor.transpose(bn_rows[half][:, s, :], bn_chunks[:, c, e, :], ident_f32[:])
-            return bn_rows
+                else:
+                    nc.vector.tensor_scalar(
+                        out=bn_chunks[:, c, e, :], in0=split[:, s, :, e], scalar1=gain, scalar2=shift,
+                        op0=ALU.mult, op1=ALU.add,
+                    )
+                nc.tensor.transpose(bn_rows[(slot, half)][:, place, :], bn_chunks[:, c, e, :], ident_f32[:])
 
-        def bn_squares(slot, bn_rows):
+        def bn_squares(slot):
             n, i = divmod(slot, GROUPS)
             for half in range(2):
                 squares = unused.tile([P, PAIRS_IN_GROUP, P], BF16, tag="squares")
                 nc.scalar.activation(
                     out=squares[:],
-                    in_=bn_rows[half][:],
+                    in_=bn_rows[(slot, half)][:],
                     func=ACT.Square,
-                    accum_out=per_bin[n]["bn_squares"][:, 2 * i + half : 2 * i + half + 1],
+                    accum_out=squares_sum[("bn", n)][:, 2 * i + half : 2 * i + half + 1],
                 )
 
         def transpose_fc(slot):
@@ -193,27 +215,28 @@ def tile_gmpahead_pb_k_kernel(tc, emb, gamma, beta, fc1d, out):
         def fc_squares(slot):
             n, i = divmod(slot, GROUPS)
             if i == 0:
-                per_bin[("fc", n)] = small.tile([P, GROUPS], F32, tag="fc_squares", name="fc_squares")
+                squares_sum[("fc", n)] = small.tile([P, GROUPS], F32, tag="fc_squares", name="fc_squares")
             squares = unused.tile([P, CHUNKS_IN_GROUP, P], BF16, tag="fc_sq")
             nc.scalar.activation(
-                out=squares[:], in_=fc_t[slot][:], func=ACT.Square, accum_out=per_bin[("fc", n)][:, i : i + 1]
+                out=squares[:], in_=fc_t[slot][:], func=ACT.Square, accum_out=squares_sum[("fc", n)][:, i : i + 1]
             )
 
-        def norm_root(sums, name):
-            norm = small.tile([P, 1], F32, tag="norm" + name, name="norm")
-            nc.vector.reduce_sum(out=norm[:], in_=sums[:], axis=mybir.AxisListType.X)
-            nc.vector.tensor_scalar_max(out=norm[:], in0=norm[:], scalar1=L2_EPS * L2_EPS)
-            nc.scalar.activation(out=norm[:], in_=norm[:], func=ACT.Sqrt)
-            return norm
+        def norm_root(name, n):
+            norm[name] = small.tile([P, 1], F32, tag="norm" + name, name="norm")
+            nc.vector.reduce_sum(out=norm[name][:], in_=squares_sum[(name, n)][:], axis=mybir.AxisListType.X)
+            nc.vector.tensor_scalar_max(out=norm[name][:], in0=norm[name][:], scalar1=L2_EPS * L2_EPS)
+            nc.scalar.activation(out=norm[name][:], in_=norm[name][:], func=ACT.Sqrt)
 
-        def spread_inverse(norm, into):
-            nc.vector.reciprocal(out=norm[:], in_=norm[:])
-            nc.tensor.matmul(into, lhsT=norm[:, 0:1].to_broadcast([P, P]), rhs=ident_f32[:], start=True, stop=True)
+        def spread_inverse(name, into):
+            nc.vector.reciprocal(out=norm[name][:], in_=norm[name][:])
+            nc.tensor.matmul(
+                into, lhsT=norm[name][:, 0:1].to_broadcast([P, P]), rhs=ident_f32[:], start=True, stop=True
+            )
 
-        def scale(engine, name, source, n, j):
+        def scale(name, source, n, j):
             passes = slice(PASSES_IN_PIECE * j, PASSES_IN_PIECE * (j + 1))
             result = grouped.tile([P, PASSES_IN_PIECE, P, PACK], BF16, tag="g" + name, name="g", align_bytes=64)
-            engine.tensor_tensor(
+            nc.vector.tensor_tensor(
                 out=result[:],
                 in0=source[:, passes, :, :].rearrange("p g t c -> p g c t"),
                 in1=inverse[(name, n)].unsqueeze(1).unsqueeze(3).to_broadcast([P, PASSES_IN_PIECE, P, PACK]),
@@ -250,64 +273,59 @@ def tile_gmpahead_pb_k_kernel(tc, emb, gamma, beta, fc1d, out):
                 nc.scalar.copy(out=logits[:, n, :], in_=acc[n][:])
                 nc.sync.dma_start(out=out[:, n, :], in_=logits[:, n, :])
 
-        def is_slot(slot):
-            return 0 <= slot < SLOTS
-
-        norms = {}
         with tc.manual_schedule():
-            for r in range(-FC_AHEAD - 1, SLOTS + GROUPS + 2):
-                n, i = divmod(r, GROUPS)
-                if is_slot(r + 2) and (r + 2) % GROUPS == 0:
-                    open_bin((r + 2) // GROUPS)
-                if i == GROUPS - 2 and 0 <= n and n + 2 < BINS:
-                    load_emb(n + 2)
-                if i == 0 and 1 <= n and n + 2 < BINS:
-                    load_fc(n + 2)
+            for r in range(-FC_AHEAD - 1, SLOTS + GROUPS + 3):
+                if first_of_bin(r + 2) is not None:
+                    open_bin(first_of_bin(r + 2))
+                if first_of_bin(r - 6) is not None and first_of_bin(r - 6) + 2 < BINS:
+                    load_emb(first_of_bin(r - 6) + 2)
+                if first_of_bin(r - 8) is not None and first_of_bin(r - 8) + 3 < BINS:
+                    load_fc(first_of_bin(r - 8) + 3)
 
-                if is_slot(r):
-                    bn_rows = batch_norm(r)
                 if is_slot(r + 2):
                     transpose_emb(r + 2)
-                if is_slot(r + 1):
-                    statistics(r + 1)
-                if is_slot(r):
-                    bn_squares(r, bn_rows)
                 if is_slot(r + FC_AHEAD):
                     fc_squares(r + FC_AHEAD)
                 if is_slot(r + FC_AHEAD + 1):
                     transpose_fc(r + FC_AHEAD + 1)
+                if is_slot(r + 1):
+                    statistics(r + 1)
+                if is_slot(r):
+                    batch_norm(r)
+                if is_slot(r + 1):
+                    deviation(r + 1)
+                if is_slot(r):
+                    bn_squares(r)
 
-                if i == 0 and 1 <= n <= BINS:
-                    norms["bn"] = norm_root(per_bin[n - 1]["bn_squares"], "bn")
-                if i == GROUPS - 1 and 0 <= n + 1 < BINS:
-                    norms["fc"] = norm_root(per_bin[("fc", n + 1)], "fc")
+                bn_bin = first_of_bin(r - GROUPS)
+                fc_bin = first_of_bin(r + FC_AHEAD - GROUPS)
+                if bn_bin is not None:
+                    norm_root("bn", bn_bin)
+                if fc_bin is not None:
+                    norm_root("fc", fc_bin)
 
-                if i % 2 == 0 and 1 <= n <= BINS and i > 0:
-                    quantise("bn", n - 1, i // 2 - 1)
-                if i == 0 and 2 <= n <= BINS + 1:
-                    quantise("bn", n - 2, PIECES - 1)
-                if i % 2 == 1 and 0 <= n < BINS:
-                    quantise("fc", n, i // 2)
-                if i % 2 == 1 and 1 <= n <= BINS:
-                    scale(nc.vector, "bn", bn_t[n - 1], n - 1, i // 2)
-                if i % 2 == 0 and 0 <= n < BINS:
-                    scale(nc.vector, "fc", fc_rows[n], n, i // 2)
+                if piece_of_bin(r + FC_AHEAD - GROUPS - 2) is not None:
+                    quantise("fc", *piece_of_bin(r + FC_AHEAD - GROUPS - 2))
+                if piece_of_bin(r - GROUPS - 2) is not None:
+                    quantise("bn", *piece_of_bin(r - GROUPS - 2))
+                    multiply(*piece_of_bin(r - GROUPS - 2))
+                if piece_of_bin(r + FC_AHEAD - GROUPS - 1) is not None:
+                    n, j = piece_of_bin(r + FC_AHEAD - GROUPS - 1)
+                    scale("fc", fc_rows[n], n, j)
+                if piece_of_bin(r - GROUPS - 1) is not None:
+                    n, j = piece_of_bin(r - GROUPS - 1)
+                    scale("bn", bn_t[n], n, j)
 
-                if i == 0 and 1 <= n <= BINS:
+                if bn_bin is not None:
                     inverse_bn = psum_one.tile([P, P], F32, tag="inverse_bn")
-                    spread_inverse(norms["bn"], inverse_bn[:])
-                    inverse[("bn", n - 1)] = inverse_bn[:]
-                if i == GROUPS - 1 and 0 <= n + 1 < BINS:
+                    spread_inverse("bn", inverse_bn[:])
+                    inverse[("bn", bn_bin)] = inverse_bn[:]
+                if fc_bin is not None:
                     inverse_ps = psum_bn.tile([P, PAIRS_IN_GROUP, P], F32, tag="bn_rows")
-                    spread_inverse(norms["fc"], inverse_ps[:, 0, :])
+                    spread_inverse("fc", inverse_ps[:, 0, :])
                     inverse_fc = small.tile([P, P], F32, tag="inverse_fc")
                     nc.scalar.copy(out=inverse_fc[:], in_=inverse_ps[:, 0, :])
-                    inverse[("fc", n + 1)] = inverse_fc[:]
+                    inverse[("fc", fc_bin)] = inverse_fc[:]
 
                 if is_slot(r + 1):
                     gain_and_shift(r + 1)
-
-                if i % 2 == 0 and 1 <= n <= BINS and i > 0:
-                    multiply(n - 1, i // 2 - 1)
-                if i == 0 and 2 <= n <= BINS + 1:
-                    multiply(n - 2, PIECES - 1)

@@ -26,7 +26,6 @@ PIECES = 4
 PASSES_IN_PIECE = PASSES // PIECES
 SLOTS = BINS * GROUPS
 FC_AHEAD = GROUPS + 1
-VECTOR_CHUNKS = 2
 BN_EPS = 1e-5
 L2_EPS = 1e-12
 
@@ -140,11 +139,10 @@ def tile_gmpahead_pb_k_kernel(tc, emb, gamma, beta, fc1d, out):
                 c = PAIRS_IN_GROUP * i + s
                 nc.tensor.transpose(emb_t[slot][:, s, :], words[:, P * c : P * (c + 1)], ident_f32[:])
 
-        def statistics(slot):
+        def statistics(slot, s):
             n, i = divmod(slot, GROUPS)
             both = emb_t[slot][:].bitcast(BF16)
-            for s in range(PAIRS_IN_GROUP):
-                nc.vector.bn_stats(out=per_bin[n]["stats"][:, PAIRS_IN_GROUP * i + s, :], in_=both[:, s, :])
+            nc.vector.bn_stats(out=per_bin[n]["stats"][:, PAIRS_IN_GROUP * i + s, :], in_=both[:, s, :])
 
         def deviation(slot):
             n, i = divmod(slot, GROUPS)
@@ -166,10 +164,12 @@ def tile_gmpahead_pb_k_kernel(tc, emb, gamma, beta, fc1d, out):
             spread = per_bin[n]["spread"][:, chunks, :]
             gain = per_bin[n]["gain"][:, chunks, :]
             shift = per_bin[n]["shift"][:, chunks, :]
-            nc.vector.reciprocal(out=spread, in_=spread)
-            nc.gpsimd.tensor_tensor(out=gain, in0=spread, in1=affine[:, n, chunks, :], op=ALU.mult)
-            nc.gpsimd.tensor_tensor(out=shift, in0=gain, in1=moments[:, :, :, 1], op=ALU.mult)
-            nc.gpsimd.tensor_tensor(out=shift, in0=affine[:, n, beta_chunks, :], in1=shift, op=ALU.subtract)
+            return (
+                lambda: nc.vector.reciprocal(out=spread, in_=spread),
+                lambda: nc.vector.tensor_tensor(out=gain, in0=spread, in1=affine[:, n, chunks, :], op=ALU.mult),
+                lambda: nc.vector.tensor_tensor(out=shift, in0=gain, in1=moments[:, :, :, 1], op=ALU.mult),
+                lambda: nc.vector.tensor_tensor(out=shift, in0=affine[:, n, beta_chunks, :], in1=shift, op=ALU.subtract),
+            )
 
         def batch_norm(slot):
             n, i = divmod(slot, GROUPS)
@@ -183,15 +183,9 @@ def tile_gmpahead_pb_k_kernel(tc, emb, gamma, beta, fc1d, out):
                     bn_rows[(slot, half)] = psum_bn.tile([P, PAIRS_IN_GROUP, P], F32, tag="bn_rows", name="bn_rows")
                 gain = per_bin[n]["gain"][:, c, e : e + 1]
                 shift = per_bin[n]["shift"][:, c, e : e + 1]
-                if q < CHUNKS_IN_GROUP - VECTOR_CHUNKS:
-                    nc.scalar.activation(
-                        out=bn_chunks[:, c, e, :], in_=split[:, s, :, e], func=ACT.Identity, bias=shift, scale=gain
-                    )
-                else:
-                    nc.vector.tensor_scalar(
-                        out=bn_chunks[:, c, e, :], in0=split[:, s, :, e], scalar1=gain, scalar2=shift,
-                        op0=ALU.mult, op1=ALU.add,
-                    )
+                nc.scalar.activation(
+                    out=bn_chunks[:, c, e, :], in_=split[:, s, :, e], func=ACT.Identity, bias=shift, scale=gain
+                )
                 nc.tensor.transpose(bn_rows[(slot, half)][:, place, :], bn_chunks[:, c, e, :], ident_f32[:])
 
         def bn_squares(slot):
@@ -221,9 +215,11 @@ def tile_gmpahead_pb_k_kernel(tc, emb, gamma, beta, fc1d, out):
                 out=squares[:], in_=fc_t[slot][:], func=ACT.Square, accum_out=squares_sum[("fc", n)][:, i : i + 1]
             )
 
-        def norm_root(name, n):
+        def sum_of_squares(name, n):
             norm[name] = small.tile([P, 1], F32, tag="norm" + name, name="norm")
             nc.vector.reduce_sum(out=norm[name][:], in_=squares_sum[(name, n)][:], axis=mybir.AxisListType.X)
+
+        def norm_root(name):
             nc.vector.tensor_scalar_max(out=norm[name][:], in0=norm[name][:], scalar1=L2_EPS * L2_EPS)
             nc.scalar.activation(out=norm[name][:], in_=norm[name][:], func=ACT.Sqrt)
 
@@ -275,40 +271,50 @@ def tile_gmpahead_pb_k_kernel(tc, emb, gamma, beta, fc1d, out):
 
         with tc.manual_schedule():
             for r in range(-FC_AHEAD - 1, SLOTS + GROUPS + 3):
-                if first_of_bin(r + 2) is not None:
-                    open_bin(first_of_bin(r + 2))
-                if first_of_bin(r - 6) is not None and first_of_bin(r - 6) + 2 < BINS:
-                    load_emb(first_of_bin(r - 6) + 2)
+                if first_of_bin(r + 3) is not None:
+                    open_bin(first_of_bin(r + 3))
+                if first_of_bin(r - 5) is not None and first_of_bin(r - 5) + 2 < BINS:
+                    load_emb(first_of_bin(r - 5) + 2)
                 if first_of_bin(r - 8) is not None and first_of_bin(r - 8) + 3 < BINS:
                     load_fc(first_of_bin(r - 8) + 3)
 
-                if is_slot(r + 2):
-                    transpose_emb(r + 2)
                 if is_slot(r + FC_AHEAD):
                     fc_squares(r + FC_AHEAD)
                 if is_slot(r + FC_AHEAD + 1):
                     transpose_fc(r + FC_AHEAD + 1)
-                if is_slot(r + 1):
-                    statistics(r + 1)
+                steps = gain_and_shift(r + 1) if is_slot(r + 1) else ()
+                for s in range(PAIRS_IN_GROUP):
+                    if is_slot(r + 1):
+                        steps[s]()
+                    if is_slot(r + 2):
+                        statistics(r + 2, s)
                 if is_slot(r):
                     batch_norm(r)
-                if is_slot(r + 1):
-                    deviation(r + 1)
+                if is_slot(r + 3):
+                    transpose_emb(r + 3)
+                if is_slot(r + 2):
+                    deviation(r + 2)
                 if is_slot(r):
                     bn_squares(r)
 
                 bn_bin = first_of_bin(r - GROUPS)
                 fc_bin = first_of_bin(r + FC_AHEAD - GROUPS)
                 if bn_bin is not None:
-                    norm_root("bn", bn_bin)
+                    sum_of_squares("bn", bn_bin)
                 if fc_bin is not None:
-                    norm_root("fc", fc_bin)
+                    sum_of_squares("fc", fc_bin)
 
                 if piece_of_bin(r + FC_AHEAD - GROUPS - 2) is not None:
                     quantise("fc", *piece_of_bin(r + FC_AHEAD - GROUPS - 2))
                 if piece_of_bin(r - GROUPS - 2) is not None:
                     quantise("bn", *piece_of_bin(r - GROUPS - 2))
                     multiply(*piece_of_bin(r - GROUPS - 2))
+
+                if bn_bin is not None:
+                    norm_root("bn")
+                if fc_bin is not None:
+                    norm_root("fc")
+
                 if piece_of_bin(r + FC_AHEAD - GROUPS - 1) is not None:
                     n, j = piece_of_bin(r + FC_AHEAD - GROUPS - 1)
                     scale("fc", fc_rows[n], n, j)
@@ -326,6 +332,3 @@ def tile_gmpahead_pb_k_kernel(tc, emb, gamma, beta, fc1d, out):
                     inverse_fc = small.tile([P, P], F32, tag="inverse_fc")
                     nc.scalar.copy(out=inverse_fc[:], in_=inverse_ps[:, 0, :])
                     inverse[("fc", fc_bin)] = inverse_fc[:]
-
-                if is_slot(r + 1):
-                    gain_and_shift(r + 1)

@@ -57,7 +57,7 @@ def tile_gmpahead_pb_k_kernel(tc, emb, gamma, beta, fc1d, out):
         unused = stack.enter_context(tc.tile_pool(name="unused", bufs=2))
         psum_emb = stack.enter_context(tc.psum_pool(name="psum_emb", bufs=3))
         psum_bn = stack.enter_context(tc.psum_pool(name="psum_bn", bufs=2))
-        psum_fc = stack.enter_context(tc.psum_pool(name="psum_fc", bufs=1))
+        psum_fc = stack.enter_context(tc.psum_pool(name="psum_fc", bufs=2))
         psum_one = stack.enter_context(tc.psum_pool(name="psum_one", bufs=1))
 
         ident_f32 = const.tile([P, P], F32)
@@ -223,11 +223,14 @@ def tile_gmpahead_pb_k_kernel(tc, emb, gamma, beta, fc1d, out):
             nc.vector.tensor_scalar_max(out=norm[name][:], in0=norm[name][:], scalar1=L2_EPS * L2_EPS)
             nc.scalar.activation(out=norm[name][:], in_=norm[name][:], func=ACT.Sqrt)
 
-        def spread_inverse(name, into):
+        def spread_inverse(name, n):
             nc.vector.reciprocal(out=norm[name][:], in_=norm[name][:])
+            spread = psum_bn.tile([P, PAIRS_IN_GROUP, P], F32, tag="bn_rows")
             nc.tensor.matmul(
-                into, lhsT=norm[name][:, 0:1].to_broadcast([P, P]), rhs=ident_f32[:], start=True, stop=True
+                spread[:, 0, :], lhsT=norm[name][:, 0:1].to_broadcast([P, P]), rhs=ident_f32[:], start=True, stop=True
             )
+            inverse[(name, n)] = small.tile([P, P], F32, tag="inverse" + name, name="inverse")
+            nc.scalar.copy(out=inverse[(name, n)][:], in_=spread[:, 0, :])
 
         def scale(name, source, n, j):
             passes = slice(PASSES_IN_PIECE * j, PASSES_IN_PIECE * (j + 1))
@@ -235,7 +238,7 @@ def tile_gmpahead_pb_k_kernel(tc, emb, gamma, beta, fc1d, out):
             nc.vector.tensor_tensor(
                 out=result[:],
                 in0=source[:, passes, :, :].rearrange("p g t c -> p g c t"),
-                in1=inverse[(name, n)].unsqueeze(1).unsqueeze(3).to_broadcast([P, PASSES_IN_PIECE, P, PACK]),
+                in1=inverse[(name, n)][:].unsqueeze(1).unsqueeze(3).to_broadcast([P, PASSES_IN_PIECE, P, PACK]),
                 op=ALU.mult,
             )
             side_by_side[(name, n, j)] = result
@@ -278,10 +281,6 @@ def tile_gmpahead_pb_k_kernel(tc, emb, gamma, beta, fc1d, out):
                 if first_of_bin(r - 8) is not None and first_of_bin(r - 8) + 3 < BINS:
                     load_fc(first_of_bin(r - 8) + 3)
 
-                if is_slot(r + FC_AHEAD):
-                    fc_squares(r + FC_AHEAD)
-                if is_slot(r + FC_AHEAD + 1):
-                    transpose_fc(r + FC_AHEAD + 1)
                 steps = gain_and_shift(r + 1) if is_slot(r + 1) else ()
                 for s in range(PAIRS_IN_GROUP):
                     if is_slot(r + 1):
@@ -292,8 +291,12 @@ def tile_gmpahead_pb_k_kernel(tc, emb, gamma, beta, fc1d, out):
                     batch_norm(r)
                 if is_slot(r + 3):
                     transpose_emb(r + 3)
+                if is_slot(r + FC_AHEAD + 1):
+                    transpose_fc(r + FC_AHEAD + 1)
                 if is_slot(r + 2):
                     deviation(r + 2)
+                if is_slot(r + FC_AHEAD):
+                    fc_squares(r + FC_AHEAD)
                 if is_slot(r):
                     bn_squares(r)
 
@@ -323,12 +326,6 @@ def tile_gmpahead_pb_k_kernel(tc, emb, gamma, beta, fc1d, out):
                     scale("bn", bn_t[n], n, j)
 
                 if bn_bin is not None:
-                    inverse_bn = psum_one.tile([P, P], F32, tag="inverse_bn")
-                    spread_inverse("bn", inverse_bn[:])
-                    inverse[("bn", bn_bin)] = inverse_bn[:]
+                    spread_inverse("bn", bn_bin)
                 if fc_bin is not None:
-                    inverse_ps = psum_bn.tile([P, PAIRS_IN_GROUP, P], F32, tag="bn_rows")
-                    spread_inverse("fc", inverse_ps[:, 0, :])
-                    inverse_fc = small.tile([P, P], F32, tag="inverse_fc")
-                    nc.scalar.copy(out=inverse_fc[:], in_=inverse_ps[:, 0, :])
-                    inverse[("fc", fc_bin)] = inverse_fc[:]
+                    spread_inverse("fc", fc_bin)

@@ -25,7 +25,7 @@ CHUNKS_IN_GROUP = CHUNKS // GROUPS
 PIECES = 4
 PASSES_IN_PIECE = PASSES // PIECES
 SLOTS = BINS * GROUPS
-FC_AHEAD = GROUPS + 1
+FC_AHEAD = GROUPS - 1
 BN_EPS = 1e-5
 L2_EPS = 1e-12
 
@@ -125,7 +125,7 @@ def tile_gmpahead_pb_k_kernel(tc, emb, gamma, beta, fc1d, out):
             bn_t[n] = bn_pool.tile([P, PASSES, PACK, P], F32, tag="bn_t", name="bn_t")
             per_bin[n] = {
                 "stats": small.tile([P, PAIRS, 6], F32, tag="stats", name="stats"),
-                "spread": small.tile([P, PAIRS, 2], F32, tag="spread", name="spread"),
+                "narrow": small.tile([P, PAIRS, 2], F32, tag="narrow", name="narrow"),
                 "gain": small.tile([P, PAIRS, 2], F32, tag="gain", name="gain"),
                 "shift": small.tile([P, PAIRS, 2], F32, tag="shift", name="shift"),
             }
@@ -149,7 +149,7 @@ def tile_gmpahead_pb_k_kernel(tc, emb, gamma, beta, fc1d, out):
             chunks = slice(PAIRS_IN_GROUP * i, PAIRS_IN_GROUP * (i + 1))
             moments = per_bin[n]["stats"][:, chunks, :].rearrange("p c (e m) -> p c e m", m=3)
             nc.scalar.activation(
-                out=per_bin[n]["spread"][:, chunks, :],
+                out=per_bin[n]["narrow"][:, chunks, :],
                 in_=moments[:, :, :, 2],
                 func=ACT.Sqrt,
                 bias=bn_eps[:],
@@ -161,13 +161,15 @@ def tile_gmpahead_pb_k_kernel(tc, emb, gamma, beta, fc1d, out):
             chunks = slice(PAIRS_IN_GROUP * i, PAIRS_IN_GROUP * (i + 1))
             beta_chunks = slice(PAIRS + PAIRS_IN_GROUP * i, PAIRS + PAIRS_IN_GROUP * (i + 1))
             moments = per_bin[n]["stats"][:, chunks, :].rearrange("p c (e m) -> p c e m", m=3)
-            spread = per_bin[n]["spread"][:, chunks, :]
+            narrow = per_bin[n]["narrow"][:, chunks, :]
             gain = per_bin[n]["gain"][:, chunks, :]
             shift = per_bin[n]["shift"][:, chunks, :]
+            mult = ALU.mult
             return (
-                lambda: nc.vector.reciprocal(out=spread, in_=spread),
-                lambda: nc.vector.tensor_tensor(out=gain, in0=spread, in1=affine[:, n, chunks, :], op=ALU.mult),
-                lambda: nc.vector.tensor_tensor(out=shift, in0=gain, in1=moments[:, :, :, 1], op=ALU.mult),
+                lambda: nc.vector.tensor_tensor(out=shift, in0=affine[:, n, chunks, :], in1=moments[:, :, :, 1], op=mult),
+                lambda: nc.vector.reciprocal(out=narrow, in_=narrow),
+                lambda: nc.vector.tensor_tensor(out=gain, in0=affine[:, n, chunks, :], in1=narrow, op=mult),
+                lambda: nc.vector.tensor_tensor(out=shift, in0=shift, in1=narrow, op=mult),
                 lambda: nc.vector.tensor_tensor(out=shift, in0=affine[:, n, beta_chunks, :], in1=shift, op=ALU.subtract),
             )
 
@@ -223,14 +225,14 @@ def tile_gmpahead_pb_k_kernel(tc, emb, gamma, beta, fc1d, out):
             nc.vector.tensor_scalar_max(out=norm[name][:], in0=norm[name][:], scalar1=L2_EPS * L2_EPS)
             nc.scalar.activation(out=norm[name][:], in_=norm[name][:], func=ACT.Sqrt)
 
-        def spread_inverse(name, n):
+        def inverse_norm(name, n):
             nc.vector.reciprocal(out=norm[name][:], in_=norm[name][:])
-            spread = psum_bn.tile([P, PAIRS_IN_GROUP, P], F32, tag="bn_rows")
+            along = psum_bn.tile([P, PAIRS_IN_GROUP, P], F32, tag="bn_rows")
             nc.tensor.matmul(
-                spread[:, 0, :], lhsT=norm[name][:, 0:1].to_broadcast([P, P]), rhs=ident_f32[:], start=True, stop=True
+                along[:, 0, :], lhsT=norm[name][:, 0:1].to_broadcast([P, P]), rhs=ident_f32[:], start=True, stop=True
             )
             inverse[(name, n)] = small.tile([P, P], F32, tag="inverse" + name, name="inverse")
-            nc.scalar.copy(out=inverse[(name, n)][:], in_=spread[:, 0, :])
+            nc.scalar.copy(out=inverse[(name, n)][:], in_=along[:, 0, :])
 
         def scale(name, source, n, j):
             passes = slice(PASSES_IN_PIECE * j, PASSES_IN_PIECE * (j + 1))
@@ -278,30 +280,30 @@ def tile_gmpahead_pb_k_kernel(tc, emb, gamma, beta, fc1d, out):
                     open_bin(first_of_bin(r + 3))
                 if first_of_bin(r - 5) is not None and first_of_bin(r - 5) + 2 < BINS:
                     load_emb(first_of_bin(r - 5) + 2)
-                if first_of_bin(r - 8) is not None and first_of_bin(r - 8) + 3 < BINS:
-                    load_fc(first_of_bin(r - 8) + 3)
+                if first_of_bin(r + FC_AHEAD - 2 * GROUPS) is not None and first_of_bin(r + FC_AHEAD - 2 * GROUPS) + 3 < BINS:
+                    load_fc(first_of_bin(r + FC_AHEAD - 2 * GROUPS) + 3)
 
-                steps = gain_and_shift(r + 1) if is_slot(r + 1) else ()
-                for s in range(PAIRS_IN_GROUP):
-                    if is_slot(r + 1):
-                        steps[s]()
-                    if is_slot(r + 2):
-                        statistics(r + 2, s)
                 if is_slot(r):
                     batch_norm(r)
                 if is_slot(r + 3):
                     transpose_emb(r + 3)
                 if is_slot(r + FC_AHEAD + 1):
                     transpose_fc(r + FC_AHEAD + 1)
-                if is_slot(r + 2):
-                    deviation(r + 2)
                 if is_slot(r + FC_AHEAD):
                     fc_squares(r + FC_AHEAD)
                 if is_slot(r):
                     bn_squares(r)
 
+                for s in range(PAIRS_IN_GROUP):
+                    if is_slot(r + 2):
+                        statistics(r + 2, s)
+                if is_slot(r + 2):
+                    deviation(r + 2)
+                steps = gain_and_shift(r + 1) if is_slot(r + 1) else ()
                 bn_bin = first_of_bin(r - GROUPS)
                 fc_bin = first_of_bin(r + FC_AHEAD - GROUPS)
+                for step in steps[0:2]:
+                    step()
                 if bn_bin is not None:
                     sum_of_squares("bn", bn_bin)
                 if fc_bin is not None:
@@ -313,6 +315,8 @@ def tile_gmpahead_pb_k_kernel(tc, emb, gamma, beta, fc1d, out):
                     quantise("bn", *piece_of_bin(r - GROUPS - 2))
                     multiply(*piece_of_bin(r - GROUPS - 2))
 
+                for step in steps[2:4]:
+                    step()
                 if bn_bin is not None:
                     norm_root("bn")
                 if fc_bin is not None:
@@ -325,7 +329,9 @@ def tile_gmpahead_pb_k_kernel(tc, emb, gamma, beta, fc1d, out):
                     n, j = piece_of_bin(r - GROUPS - 1)
                     scale("bn", bn_t[n], n, j)
 
+                for step in steps[4:5]:
+                    step()
                 if bn_bin is not None:
-                    spread_inverse("bn", bn_bin)
+                    inverse_norm("bn", bn_bin)
                 if fc_bin is not None:
-                    spread_inverse("fc", fc_bin)
+                    inverse_norm("fc", fc_bin)

@@ -26,6 +26,7 @@ PIECES = 4
 PASSES_IN_PIECE = PASSES // PIECES
 SLOTS = BINS * GROUPS
 FC_AHEAD = GROUPS - 1
+RUN = 4
 BN_EPS = 1e-5
 L2_EPS = 1e-12
 
@@ -235,14 +236,15 @@ def tile_gmpahead_pb_k_kernel(tc, emb, gamma, beta, fc1d, out):
             nc.scalar.copy(out=inverse[(name, n)][:], in_=along[:, 0, :])
 
         def scale(name, source, n, j):
-            passes = slice(PASSES_IN_PIECE * j, PASSES_IN_PIECE * (j + 1))
             result = grouped.tile([P, PASSES_IN_PIECE, P, PACK], BF16, tag="g" + name, name="g", align_bytes=64)
-            nc.vector.tensor_tensor(
-                out=result[:],
-                in0=source[:, passes, :, :].rearrange("p g t c -> p g c t"),
-                in1=inverse[(name, n)][:].unsqueeze(1).unsqueeze(3).to_broadcast([P, PASSES_IN_PIECE, P, PACK]),
-                op=ALU.mult,
-            )
+            along = inverse[(name, n)][:].rearrange("p (c i) -> p c i", i=RUN)
+            for g in range(PASSES_IN_PIECE):
+                nc.vector.tensor_tensor(
+                    out=result[:, g, :, :].rearrange("p (c i) t -> p c t i", i=RUN),
+                    in0=source[:, PASSES_IN_PIECE * j + g, :, :].rearrange("p t (c i) -> p c t i", i=RUN),
+                    in1=along.unsqueeze(2).to_broadcast([P, P // RUN, PACK, RUN]),
+                    op=ALU.mult,
+                )
             side_by_side[(name, n, j)] = result
 
         def quantise(name, n, j):

@@ -16,67 +16,75 @@ P = 128
 BINS = 7
 FEATURES = 8192
 PACK = 4
-PASSES = FEATURES // (P * PACK)
-PAIRS = FEATURES // (2 * P)
-CHUNKS = FEATURES // P
 GROUPS = 8
-PAIRS_IN_GROUP = PAIRS // GROUPS
-CHUNKS_IN_GROUP = CHUNKS // GROUPS
-PIECES = 4
-PASSES_IN_PIECE = PASSES // PIECES
 SLOTS = BINS * GROUPS
-FC_AHEAD = GROUPS - 1
+SLOT_FEATURES = FEATURES // GROUPS
+PASSES = SLOT_FEATURES // (P * PACK)
+PAIRS = SLOT_FEATURES // (2 * P)
+CHUNKS = SLOT_FEATURES // P
+BIN_PAIRS = GROUPS * PAIRS
 RUN = 4
 BN_EPS = 1e-5
 L2_EPS = 1e-12
 
 FLOPS = 2 * BINS * P * FEATURES * P
 
+LOAD_EMB = -8
+LOAD_FC = -7
+TURN_FOR_STATS = -1
+STATS = 0
+GAIN = STATS + 1
+TURN_FOR_BN = STATS + GROUPS
+BN = TURN_FOR_BN + 1
+ADD_BN_SQUARES = BN + 1
+BN_NORM = ADD_BN_SQUARES + 1
+SCALE_BN = ADD_BN_SQUARES + GROUPS + 3
+FC_SQUARES = 0
+ADD_FC_SQUARES = FC_SQUARES + 1
+FC_NORM = ADD_FC_SQUARES + 1
+SCALE_FC = ADD_FC_SQUARES + GROUPS + 3
+MULTIPLY = SCALE_BN + 1
+
 
 def is_slot(k):
     return 0 <= k < SLOTS
 
 
-def first_of_bin(k):
-    return k // GROUPS if is_slot(k) and k % GROUPS == 0 else None
-
-
-def piece_of_bin(k):
-    return (k // GROUPS, k % GROUPS // 2) if is_slot(k) and k % 2 == 0 else None
+def bin_ended_by(k):
+    return k // GROUPS if is_slot(k) and k % GROUPS == GROUPS - 1 else None
 
 
 def tile_gmpahead_pb_k_kernel(tc, emb, gamma, beta, fc1d, out):
     nc = tc.nc
     with ExitStack() as stack:
         const = stack.enter_context(tc.tile_pool(name="const", bufs=1))
-        emb_pool = stack.enter_context(tc.tile_pool(name="emb", bufs=2))
-        fc_pool = stack.enter_context(tc.tile_pool(name="fc", bufs=3))
-        bn_pool = stack.enter_context(tc.tile_pool(name="bn", bufs=2))
+        emb_pool = stack.enter_context(tc.tile_pool(name="emb", bufs=TURN_FOR_BN - LOAD_EMB + 1))
+        fc_pool = stack.enter_context(tc.tile_pool(name="fc", bufs=SCALE_FC - LOAD_FC + 1))
+        bn_pool = stack.enter_context(tc.tile_pool(name="bn", bufs=SCALE_BN - BN + 2))
         small = stack.enter_context(tc.tile_pool(name="small", bufs=2))
+        squares_pool = stack.enter_context(tc.tile_pool(name="squares", bufs=2))
         grouped = stack.enter_context(tc.tile_pool(name="grouped", bufs=2))
-        packed = stack.enter_context(tc.tile_pool(name="packed", bufs=2))
-        unused = stack.enter_context(tc.tile_pool(name="unused", bufs=2))
-        psum_emb = stack.enter_context(tc.psum_pool(name="psum_emb", bufs=3))
-        psum_bn = stack.enter_context(tc.psum_pool(name="psum_bn", bufs=2))
-        psum_fc = stack.enter_context(tc.psum_pool(name="psum_fc", bufs=2))
-        psum_one = stack.enter_context(tc.psum_pool(name="psum_one", bufs=1))
+        bn_packed = stack.enter_context(tc.tile_pool(name="bn_packed", bufs=3))
+        fc_packed = stack.enter_context(tc.tile_pool(name="fc_packed", bufs=MULTIPLY - SCALE_FC + 2))
+        psum_turned = stack.enter_context(tc.psum_pool(name="psum_turned", bufs=5))
+        psum_bn = stack.enter_context(tc.psum_pool(name="psum_bn", bufs=1))
+        psum_fc = stack.enter_context(tc.psum_pool(name="psum_fc", bufs=1))
+        psum_mx = stack.enter_context(tc.psum_pool(name="psum_mx", bufs=1))
 
         ident_f32 = const.tile([P, P], F32)
         make_identity(nc, ident_f32[:])
-        ident_bf16 = const.tile([P, P], BF16)
-        make_identity(nc, ident_bf16[:])
         bn_eps = const.tile([P, 1], F32)
         nc.vector.memset(bn_eps[:], BN_EPS)
         logits = const.tile([P, BINS, P], F32)
 
         emb_rows = {}
         fc_rows = {}
+        for_stats = {}
+        for_bn = {}
         bn_t = {}
         per_bin = {}
-        squares_sum = {}
-        emb_t = {}
-        bn_rows = {}
-        fc_t = {}
+        squares = {}
+        sums = {}
         norm = {}
         inverse = {}
         side_by_side = {}
@@ -84,256 +92,268 @@ def tile_gmpahead_pb_k_kernel(tc, emb, gamma, beta, fc1d, out):
         scales = {}
         acc = {}
 
-        def load_emb(n):
-            emb_rows[n] = emb_pool.tile([P, FEATURES], BF16, tag="emb_rows", name="emb_rows")
-            quarter = FEATURES // 4
-            for q in range(4):
-                cols = slice(quarter * q, quarter * (q + 1))
-                nc.sync.dma_start(out=emb_rows[n][:, cols], in_=emb[n][:, cols])
+        def load_emb(k):
+            n, i = divmod(k, GROUPS)
+            emb_rows[k] = emb_pool.tile([P, SLOT_FEATURES], BF16, tag="emb_rows", name="emb_rows")
+            nc.sync.dma_start(out=emb_rows[k][:], in_=emb[n][:, SLOT_FEATURES * i : SLOT_FEATURES * (i + 1)])
 
-        def load_fc(n):
-            fc_rows[n] = fc_pool.tile([P, PASSES, PACK, P], BF16, tag="fc_rows", name="fc_rows")
-            into = fc_rows[n][:].rearrange("p g (u e) k -> p (g u) (e k)", e=2)
-            source = fc1d[n].rearrange("(c p e) k -> p c (e k)", p=P, e=2)
-            quarter = PAIRS // 4
-            for q in range(4):
-                some = slice(quarter * q, quarter * (q + 1))
-                nc.sync.dma_start(out=into[:, some, :], in_=source[:, some, :])
+        def load_fc(k):
+            n, i = divmod(k, GROUPS)
+            fc_rows[k] = fc_pool.tile([P, PASSES, PACK, P], BF16, tag="fc_rows", name="fc_rows")
+            nc.sync.dma_start(
+                out=fc_rows[k][:].rearrange("p g (u e) k -> p (g u) (e k)", e=2),
+                in_=fc1d[n][SLOT_FEATURES * i : SLOT_FEATURES * (i + 1), :].rearrange("(c p e) k -> p c (e k)", p=P, e=2),
+            )
 
-        load_fc(0)
-        load_emb(0)
+        def turn(k):
+            turned = psum_turned.tile([P, PAIRS, P], F32, tag="turned", name="turned")
+            words = emb_rows[k][:].bitcast(F32)
+            for s in range(PAIRS):
+                nc.tensor.transpose(turned[:, s, :], words[:, P * s : P * (s + 1)], ident_f32[:])
+            return turned
 
         affine_rows = const.tile([P, BINS, 2 * P], BF16)
         nc.vector.memset(affine_rows[64:128, :, :].bitcast(I32), 0)
         nc.scalar.dma_start(out=affine_rows[0:32, :, :], in_=gamma.rearrange("n (c x) -> c n x", x=2 * P))
         nc.scalar.dma_start(out=affine_rows[32:64, :, :], in_=beta.rearrange("n (c x) -> c n x", x=2 * P))
-        affine = const.tile([P, BINS, 2 * PAIRS, 2], F32)
-        for first in range(0, BINS, PAIRS_IN_GROUP):
-            count = min(PAIRS_IN_GROUP, BINS - first)
-            flipped = psum_emb.tile([P, PAIRS_IN_GROUP, P], F32, tag="emb_t")
-            for s in range(count):
-                nc.tensor.transpose(flipped[:, s, :], affine_rows[:, first + s, :].bitcast(F32), ident_f32[:])
-            pairs = flipped[:].bitcast(BF16).rearrange("p s (r e) -> p s r e", e=2)
-            nc.vector.tensor_copy(
-                out=affine[:, first : first + count, :, :], in_=pairs[:, 0:count, 0 : 2 * PAIRS, :]
-            )
+        affine = const.tile([P, BINS, 2 * BIN_PAIRS, 2], F32)
 
-        load_fc(1)
-        load_emb(1)
-        load_fc(2)
+        def turn_affine():
+            for first in range(0, BINS, PAIRS):
+                count = min(PAIRS, BINS - first)
+                flipped = psum_turned.tile([P, PAIRS, P], F32, tag="turned")
+                for s in range(count):
+                    nc.tensor.transpose(flipped[:, s, :], affine_rows[:, first + s, :].bitcast(F32), ident_f32[:])
+                pairs = flipped[:].bitcast(BF16).rearrange("p s (r e) -> p s r e", e=2)
+                nc.vector.tensor_copy(
+                    out=affine[:, first : first + count, :, :], in_=pairs[:, 0:count, 0 : 2 * BIN_PAIRS, :]
+                )
 
         def open_bin(n):
-            bn_t[n] = bn_pool.tile([P, PASSES, PACK, P], F32, tag="bn_t", name="bn_t")
             per_bin[n] = {
-                "stats": small.tile([P, PAIRS, 6], F32, tag="stats", name="stats"),
-                "narrow": small.tile([P, PAIRS, 2], F32, tag="narrow", name="narrow"),
-                "gain": small.tile([P, PAIRS, 2], F32, tag="gain", name="gain"),
-                "shift": small.tile([P, PAIRS, 2], F32, tag="shift", name="shift"),
+                "stats": small.tile([P, BIN_PAIRS, 6], F32, tag="stats", name="stats"),
+                "narrow": small.tile([P, BIN_PAIRS, 2], F32, tag="narrow", name="narrow"),
+                "gain": small.tile([P, BIN_PAIRS, 2], F32, tag="gain", name="gain"),
+                "shift": small.tile([P, BIN_PAIRS, 2], F32, tag="shift", name="shift"),
             }
-            squares_sum[("bn", n)] = small.tile([P, 2 * GROUPS], F32, tag="bn_squares", name="bn_squares")
 
-        def transpose_emb(slot):
-            n, i = divmod(slot, GROUPS)
-            words = emb_rows[n][:].bitcast(F32)
-            emb_t[slot] = psum_emb.tile([P, PAIRS_IN_GROUP, P], F32, tag="emb_t", name="emb_t")
-            for s in range(PAIRS_IN_GROUP):
-                c = PAIRS_IN_GROUP * i + s
-                nc.tensor.transpose(emb_t[slot][:, s, :], words[:, P * c : P * (c + 1)], ident_f32[:])
+        def statistics(k, s):
+            n, i = divmod(k, GROUPS)
+            both = for_stats[k][:].bitcast(BF16)
+            nc.vector.bn_stats(out=per_bin[n]["stats"][:, PAIRS * i + s, :], in_=both[:, s, :])
 
-        def statistics(slot, s):
-            n, i = divmod(slot, GROUPS)
-            both = emb_t[slot][:].bitcast(BF16)
-            nc.vector.bn_stats(out=per_bin[n]["stats"][:, PAIRS_IN_GROUP * i + s, :], in_=both[:, s, :])
-
-        def deviation(slot):
-            n, i = divmod(slot, GROUPS)
-            chunks = slice(PAIRS_IN_GROUP * i, PAIRS_IN_GROUP * (i + 1))
-            moments = per_bin[n]["stats"][:, chunks, :].rearrange("p c (e m) -> p c e m", m=3)
+        def deviation(n):
+            moments = per_bin[n]["stats"][:].rearrange("p c (e m) -> p c e m", m=3)
             nc.scalar.activation(
-                out=per_bin[n]["narrow"][:, chunks, :],
+                out=per_bin[n]["narrow"][:],
                 in_=moments[:, :, :, 2],
                 func=ACT.Sqrt,
                 bias=bn_eps[:],
                 scale=1.0 / P,
             )
 
-        def gain_and_shift(slot):
-            n, i = divmod(slot, GROUPS)
-            chunks = slice(PAIRS_IN_GROUP * i, PAIRS_IN_GROUP * (i + 1))
-            beta_chunks = slice(PAIRS + PAIRS_IN_GROUP * i, PAIRS + PAIRS_IN_GROUP * (i + 1))
-            moments = per_bin[n]["stats"][:, chunks, :].rearrange("p c (e m) -> p c e m", m=3)
-            narrow = per_bin[n]["narrow"][:, chunks, :]
-            gain = per_bin[n]["gain"][:, chunks, :]
-            shift = per_bin[n]["shift"][:, chunks, :]
+        def gain_and_shift(n):
+            moments = per_bin[n]["stats"][:].rearrange("p c (e m) -> p c e m", m=3)
+            narrow = per_bin[n]["narrow"][:]
+            gain = per_bin[n]["gain"][:]
+            shift = per_bin[n]["shift"][:]
+            gammas = affine[:, n, 0:BIN_PAIRS, :]
+            betas = affine[:, n, BIN_PAIRS : 2 * BIN_PAIRS, :]
             mult = ALU.mult
-            return (
-                lambda: nc.vector.tensor_tensor(out=shift, in0=affine[:, n, chunks, :], in1=moments[:, :, :, 1], op=mult),
+            return [
+                lambda: nc.vector.tensor_tensor(out=shift, in0=gammas, in1=moments[:, :, :, 1], op=mult),
                 lambda: nc.vector.reciprocal(out=narrow, in_=narrow),
-                lambda: nc.vector.tensor_tensor(out=gain, in0=affine[:, n, chunks, :], in1=narrow, op=mult),
+                lambda: nc.vector.tensor_tensor(out=gain, in0=gammas, in1=narrow, op=mult),
                 lambda: nc.vector.tensor_tensor(out=shift, in0=shift, in1=narrow, op=mult),
-                lambda: nc.vector.tensor_tensor(out=shift, in0=affine[:, n, beta_chunks, :], in1=shift, op=ALU.subtract),
-            )
+                lambda: nc.vector.tensor_tensor(out=shift, in0=betas, in1=shift, op=ALU.subtract),
+            ]
 
-        def batch_norm(slot):
-            n, i = divmod(slot, GROUPS)
-            split = emb_t[slot][:].bitcast(BF16).rearrange("p s (b e) -> p s b e", e=2)
-            bn_chunks = bn_t[n][:].rearrange("p g (u e) b -> p (g u) e b", e=2)
-            for q in range(CHUNKS_IN_GROUP):
-                half, place = divmod(q, PAIRS_IN_GROUP)
-                s, e = divmod(q, 2)
-                c = PAIRS_IN_GROUP * i + s
-                if place == 0:
-                    bn_rows[(slot, half)] = psum_bn.tile([P, PAIRS_IN_GROUP, P], F32, tag="bn_rows", name="bn_rows")
-                gain = per_bin[n]["gain"][:, c, e : e + 1]
-                shift = per_bin[n]["shift"][:, c, e : e + 1]
-                nc.scalar.activation(
-                    out=bn_chunks[:, c, e, :], in_=split[:, s, :, e], func=ACT.Identity, bias=shift, scale=gain
-                )
-                nc.tensor.transpose(bn_rows[(slot, half)][:, place, :], bn_chunks[:, c, e, :], ident_f32[:])
+        def batch_norm(k):
+            n, i = divmod(k, GROUPS)
+            split = for_bn[k][:].bitcast(BF16).rearrange("p s (b e) -> p s b e", e=2)
+            bn_t[k] = bn_pool.tile([P, PASSES, PACK, P], F32, tag="bn_t", name="bn_t")
+            chunks = bn_t[k][:].rearrange("p g (u e) b -> p (g u) e b", e=2)
+            for s in range(PAIRS):
+                for e in range(2):
+                    nc.scalar.activation(
+                        out=chunks[:, s, e, :],
+                        in_=split[:, s, :, e],
+                        func=ACT.Identity,
+                        bias=per_bin[n]["shift"][:, PAIRS * i + s, e : e + 1],
+                        scale=per_bin[n]["gain"][:, PAIRS * i + s, e : e + 1],
+                    )
 
-        def bn_squares(slot):
-            n, i = divmod(slot, GROUPS)
-            for half in range(2):
-                squares = unused.tile([P, PAIRS_IN_GROUP, P], BF16, tag="squares")
-                nc.scalar.activation(
-                    out=squares[:],
-                    in_=bn_rows[(slot, half)][:],
-                    func=ACT.Square,
-                    accum_out=squares_sum[("bn", n)][:, 2 * i + half : 2 * i + half + 1],
-                )
-
-        def transpose_fc(slot):
-            n, i = divmod(slot, GROUPS)
-            fc_chunks = fc_rows[n][:].rearrange("p g t k -> p (g t) k")
-            fc_t[slot] = psum_fc.tile([P, CHUNKS_IN_GROUP, P], BF16, tag="fc_t", name="fc_t")
-            for s in range(CHUNKS_IN_GROUP):
-                nc.tensor.transpose(fc_t[slot][:, s, :], fc_chunks[:, CHUNKS_IN_GROUP * i + s, :], ident_bf16[:])
-
-        def fc_squares(slot):
-            n, i = divmod(slot, GROUPS)
-            if i == 0:
-                squares_sum[("fc", n)] = small.tile([P, GROUPS], F32, tag="fc_squares", name="fc_squares")
-            squares = unused.tile([P, CHUNKS_IN_GROUP, P], BF16, tag="fc_sq")
+        def square(name, source, k):
+            squares[(name, k)] = squares_pool.tile([P, CHUNKS, P], F32, tag=name + "_squares", name="squares")
             nc.scalar.activation(
-                out=squares[:], in_=fc_t[slot][:], func=ACT.Square, accum_out=squares_sum[("fc", n)][:, i : i + 1]
+                out=squares[(name, k)][:], in_=source[:].rearrange("p g t c -> p (g t) c"), func=ACT.Square
             )
+
+        def add_squares(name, pool, k):
+            n, i = divmod(k, GROUPS)
+            if i == 0:
+                sums[(name, n)] = pool.tile([P, PAIRS, P], F32, tag="sums_" + name, name="sums")
+            for q in range(CHUNKS):
+                nc.tensor.matmul(
+                    sums[(name, n)][:, 0, :],
+                    lhsT=squares[(name, k)][:, q, :],
+                    rhs=ident_f32[:],
+                    is_transpose=True,
+                    start=(i == 0 and q == 0),
+                    stop=(i == GROUPS - 1 and q == CHUNKS - 1),
+                )
 
         def sum_of_squares(name, n):
-            norm[name] = small.tile([P, 1], F32, tag="norm" + name, name="norm")
-            nc.vector.reduce_sum(out=norm[name][:], in_=squares_sum[(name, n)][:], axis=mybir.AxisListType.X)
+            norm[(name, n)] = small.tile([P, 1], F32, tag="norm" + name, name="norm")
+            one = norm[(name, n)][:]
+            return [
+                lambda: nc.vector.reduce_sum(out=one, in_=sums[(name, n)][:, 0, :], axis=mybir.AxisListType.X),
+                lambda: nc.vector.tensor_scalar_max(out=one, in0=one, scalar1=L2_EPS * L2_EPS),
+            ]
 
-        def norm_root(name):
-            nc.vector.tensor_scalar_max(out=norm[name][:], in0=norm[name][:], scalar1=L2_EPS * L2_EPS)
-            nc.scalar.activation(out=norm[name][:], in_=norm[name][:], func=ACT.Sqrt)
+        def norm_root(name, n):
+            nc.scalar.activation(out=norm[(name, n)][:], in_=norm[(name, n)][:], func=ACT.Sqrt)
 
         def inverse_norm(name, n):
-            nc.vector.reciprocal(out=norm[name][:], in_=norm[name][:])
-            along = psum_bn.tile([P, PAIRS_IN_GROUP, P], F32, tag="bn_rows")
+            one = norm[(name, n)][:]
+            return [lambda: nc.vector.reciprocal(out=one, in_=one)]
+
+        def lay_along(name, n):
+            along = psum_turned.tile([P, PAIRS, P], F32, tag="turned")
             nc.tensor.matmul(
-                along[:, 0, :], lhsT=norm[name][:, 0:1].to_broadcast([P, P]), rhs=ident_f32[:], start=True, stop=True
+                along[:, 0, :],
+                lhsT=norm[(name, n)][:, 0:1].to_broadcast([P, P]),
+                rhs=ident_f32[:],
+                start=True,
+                stop=True,
             )
             inverse[(name, n)] = small.tile([P, P], F32, tag="inverse" + name, name="inverse")
             nc.scalar.copy(out=inverse[(name, n)][:], in_=along[:, 0, :])
 
-        def scale(name, source, n, j):
-            result = grouped.tile([P, PASSES_IN_PIECE, P, PACK], BF16, tag="g" + name, name="g", align_bytes=64)
-            along = inverse[(name, n)][:].rearrange("p (c i) -> p c i", i=RUN)
-            for g in range(PASSES_IN_PIECE):
-                nc.vector.tensor_tensor(
-                    out=result[:, g, :, :].rearrange("p (c i) t -> p c t i", i=RUN),
-                    in0=source[:, PASSES_IN_PIECE * j + g, :, :].rearrange("p t (c i) -> p c t i", i=RUN),
-                    in1=along.unsqueeze(2).to_broadcast([P, P // RUN, PACK, RUN]),
-                    op=ALU.mult,
-                )
-            side_by_side[(name, n, j)] = result
-
-        def quantise(name, n, j):
-            if j == 0:
-                codes[(name, n)] = packed.tile([P, PASSES * P], U32, tag="c" + name, name="c", align_bytes=64)
-                scales[(name, n)] = packed.tile([P, PASSES * P], U8, tag="s" + name, name="s", align_bytes=64)
-            cols = slice(PASSES_IN_PIECE * P * j, PASSES_IN_PIECE * P * (j + 1))
-            nc.vector.quantize_mx(
-                out=codes[(name, n)][:, cols].bitcast(FP8X4),
-                scales=scales[(name, n)][:, cols],
-                in_=side_by_side[(name, n, j)][:].rearrange("p g c t -> p (g c t)"),
+        def scale(name, source, k, g):
+            if g == 0:
+                side_by_side[(name, k)] = grouped.tile([P, PASSES, P, PACK], BF16, tag="g" + name, name="g", align_bytes=64)
+            along = inverse[(name, k // GROUPS)][:].rearrange("p (c i) -> p c i", i=RUN)
+            nc.vector.tensor_tensor(
+                out=side_by_side[(name, k)][:, g, :, :].rearrange("p (c i) t -> p c t i", i=RUN),
+                in0=source[:, g, :, :].rearrange("p t (c i) -> p c t i", i=RUN),
+                in1=along.unsqueeze(2).to_broadcast([P, P // RUN, PACK, RUN]),
+                op=ALU.mult,
             )
 
-        def multiply(n, j):
-            if j == 0:
-                acc[n] = psum_one.tile([P, P], F32, tag="acc", name="acc")
-            for g in range(PASSES_IN_PIECE * j, PASSES_IN_PIECE * (j + 1)):
+        def quantise(name, pool, k):
+            codes[(name, k)] = pool.tile([P, PASSES * P], U32, tag="c" + name, name="c", align_bytes=64)
+            scales[(name, k)] = pool.tile([P, PASSES * P], U8, tag="s" + name, name="s", align_bytes=64)
+            nc.vector.quantize_mx(
+                out=codes[(name, k)][:].bitcast(FP8X4),
+                scales=scales[(name, k)][:],
+                in_=side_by_side[(name, k)][:].rearrange("p g c t -> p (g c t)"),
+            )
+
+        def multiply(k):
+            n, i = divmod(k, GROUPS)
+            if i == 0:
+                acc[n] = psum_mx.tile([P, PAIRS, P], F32, tag="acc", name="acc")
+            for g in range(PASSES):
                 one = slice(P * g, P * (g + 1))
                 nc.tensor.matmul_mx(
-                    out=acc[n][:],
-                    lhsT=codes[("bn", n)][:, one].bitcast(FP8X4),
-                    lhsT_scale=scales[("bn", n)][:, one],
-                    rhs=codes[("fc", n)][:, one].bitcast(FP8X4),
-                    rhs_scale=scales[("fc", n)][:, one],
-                    start=(g == 0),
-                    stop=(g == PASSES - 1),
+                    out=acc[n][:, 0, :],
+                    lhsT=codes[("bn", k)][:, one].bitcast(FP8X4),
+                    lhsT_scale=scales[("bn", k)][:, one],
+                    rhs=codes[("fc", k)][:, one].bitcast(FP8X4),
+                    rhs_scale=scales[("fc", k)][:, one],
+                    start=(i == 0 and g == 0),
+                    stop=(i == GROUPS - 1 and g == PASSES - 1),
                 )
-            if j == PIECES - 1:
-                nc.scalar.copy(out=logits[:, n, :], in_=acc[n][:])
+            if i == GROUPS - 1:
+                nc.scalar.copy(out=logits[:, n, :], in_=acc[n][:, 0, :])
                 nc.sync.dma_start(out=out[:, n, :], in_=logits[:, n, :])
 
+        def one_round(r):
+            if is_slot(r - LOAD_EMB):
+                load_emb(r - LOAD_EMB)
+            if is_slot(r - LOAD_FC):
+                load_fc(r - LOAD_FC)
+
+            fc_bin = bin_ended_by(r - FC_NORM - 2)
+            if fc_bin is not None:
+                lay_along("fc", fc_bin)
+            bn_bin = bin_ended_by(r - BN_NORM - 2)
+            if bn_bin is not None:
+                lay_along("bn", bn_bin)
+            k = r - TURN_FOR_STATS
+            if is_slot(k):
+                if k % GROUPS == 0:
+                    open_bin(k // GROUPS)
+                for_stats[k] = turn(k)
+            k = r - TURN_FOR_BN
+            if is_slot(k):
+                for_bn[k] = turn(k)
+            if is_slot(r - ADD_FC_SQUARES):
+                add_squares("fc", psum_fc, r - ADD_FC_SQUARES)
+            if is_slot(r - ADD_BN_SQUARES):
+                add_squares("bn", psum_bn, r - ADD_BN_SQUARES)
+            if is_slot(r - MULTIPLY):
+                multiply(r - MULTIPLY)
+
+            gain_bin = bin_ended_by(r - GAIN)
+            if gain_bin is not None:
+                deviation(gain_bin)
+            fc_root = bin_ended_by(r - FC_NORM - 1)
+            if fc_root is not None:
+                norm_root("fc", fc_root)
+            bn_root = bin_ended_by(r - BN_NORM - 1)
+            if bn_root is not None:
+                norm_root("bn", bn_root)
+            if is_slot(r - BN):
+                batch_norm(r - BN)
+            if is_slot(r - FC_SQUARES):
+                square("fc", fc_rows[r - FC_SQUARES], r - FC_SQUARES)
+            if is_slot(r - BN):
+                square("bn", bn_t[r - BN], r - BN)
+
+            long_steps = []
+            k = r - SCALE_BN
+            if is_slot(k):
+                long_steps.extend([lambda g=g, k=k: scale("bn", bn_t[k], k, g) for g in range(PASSES)])
+            k = r - STATS
+            if is_slot(k):
+                long_steps.extend([lambda s=s, k=k: statistics(k, s) for s in range(PAIRS // 2)])
+            k = r - SCALE_FC
+            if is_slot(k):
+                long_steps.extend([lambda g=g, k=k: scale("fc", fc_rows[k], k, g) for g in range(PASSES)])
+            k = r - SCALE_BN
+            if is_slot(k):
+                long_steps.append(lambda k=k: quantise("bn", bn_packed, k))
+            k = r - STATS
+            if is_slot(k):
+                long_steps.extend([lambda s=s, k=k: statistics(k, s) for s in range(PAIRS // 2, PAIRS)])
+            k = r - SCALE_FC
+            if is_slot(k):
+                long_steps.append(lambda k=k: quantise("fc", fc_packed, k))
+
+            short_steps = []
+            if gain_bin is not None:
+                short_steps.extend(gain_and_shift(gain_bin))
+            fc_bin = bin_ended_by(r - FC_NORM)
+            if fc_bin is not None:
+                short_steps.extend(sum_of_squares("fc", fc_bin))
+            bn_bin = bin_ended_by(r - BN_NORM)
+            if bn_bin is not None:
+                short_steps.extend(sum_of_squares("bn", bn_bin))
+            if fc_root is not None:
+                short_steps.extend(inverse_norm("fc", fc_root))
+            if bn_root is not None:
+                short_steps.extend(inverse_norm("bn", bn_root))
+            for place in range(max(len(long_steps), len(short_steps))):
+                if place < len(long_steps):
+                    long_steps[place]()
+                if place < len(short_steps):
+                    short_steps[place]()
+
         with tc.manual_schedule():
-            for r in range(-FC_AHEAD - 1, SLOTS + GROUPS + 3):
-                if first_of_bin(r + 3) is not None:
-                    open_bin(first_of_bin(r + 3))
-                if first_of_bin(r - 5) is not None and first_of_bin(r - 5) + 2 < BINS:
-                    load_emb(first_of_bin(r - 5) + 2)
-                if first_of_bin(r + FC_AHEAD - 2 * GROUPS) is not None and first_of_bin(r + FC_AHEAD - 2 * GROUPS) + 3 < BINS:
-                    load_fc(first_of_bin(r + FC_AHEAD - 2 * GROUPS) + 3)
-
-                if is_slot(r):
-                    batch_norm(r)
-                if is_slot(r + 3):
-                    transpose_emb(r + 3)
-                if is_slot(r + FC_AHEAD + 1):
-                    transpose_fc(r + FC_AHEAD + 1)
-                if is_slot(r + FC_AHEAD):
-                    fc_squares(r + FC_AHEAD)
-                if is_slot(r):
-                    bn_squares(r)
-
-                for s in range(PAIRS_IN_GROUP):
-                    if is_slot(r + 2):
-                        statistics(r + 2, s)
-                if is_slot(r + 2):
-                    deviation(r + 2)
-                steps = gain_and_shift(r + 1) if is_slot(r + 1) else ()
-                bn_bin = first_of_bin(r - GROUPS)
-                fc_bin = first_of_bin(r + FC_AHEAD - GROUPS)
-                for step in steps[0:2]:
-                    step()
-                if bn_bin is not None:
-                    sum_of_squares("bn", bn_bin)
-                if fc_bin is not None:
-                    sum_of_squares("fc", fc_bin)
-
-                if piece_of_bin(r + FC_AHEAD - GROUPS - 2) is not None:
-                    quantise("fc", *piece_of_bin(r + FC_AHEAD - GROUPS - 2))
-                if piece_of_bin(r - GROUPS - 2) is not None:
-                    quantise("bn", *piece_of_bin(r - GROUPS - 2))
-                    multiply(*piece_of_bin(r - GROUPS - 2))
-
-                for step in steps[2:4]:
-                    step()
-                if bn_bin is not None:
-                    norm_root("bn")
-                if fc_bin is not None:
-                    norm_root("fc")
-
-                if piece_of_bin(r + FC_AHEAD - GROUPS - 1) is not None:
-                    n, j = piece_of_bin(r + FC_AHEAD - GROUPS - 1)
-                    scale("fc", fc_rows[n], n, j)
-                if piece_of_bin(r - GROUPS - 1) is not None:
-                    n, j = piece_of_bin(r - GROUPS - 1)
-                    scale("bn", bn_t[n], n, j)
-
-                for step in steps[4:5]:
-                    step()
-                if bn_bin is not None:
-                    inverse_norm("bn", bn_bin)
-                if fc_bin is not None:
-                    inverse_norm("fc", fc_bin)
+            for r in range(LOAD_EMB, STATS + TURN_FOR_STATS):
+                one_round(r)
+            turn_affine()
+            for r in range(STATS + TURN_FOR_STATS, SLOTS + MULTIPLY):
+                one_round(r)

@@ -63,7 +63,7 @@ def tile_gmpahead_pb_k_kernel(tc, emb, gamma, beta, fc1d, out):
         bn_pool = stack.enter_context(tc.tile_pool(name="bn", bufs=SCALE_BN - BN + 2))
         small = stack.enter_context(tc.tile_pool(name="small", bufs=2))
         squares_pool = stack.enter_context(tc.tile_pool(name="squares", bufs=2))
-        grouped = stack.enter_context(tc.tile_pool(name="grouped", bufs=2))
+        grouped = stack.enter_context(tc.tile_pool(name="grouped", bufs=1))
         bn_packed = stack.enter_context(tc.tile_pool(name="bn_packed", bufs=3))
         fc_packed = stack.enter_context(tc.tile_pool(name="fc_packed", bufs=MULTIPLY - SCALE_FC + 2))
         psum_turned = stack.enter_context(tc.psum_pool(name="psum_turned", bufs=5))
@@ -230,14 +230,23 @@ def tile_gmpahead_pb_k_kernel(tc, emb, gamma, beta, fc1d, out):
             inverse[(name, n)] = small.tile([P, P], F32, tag="inverse" + name, name="inverse")
             nc.scalar.copy(out=inverse[(name, n)][:], in_=along[:, 0, :])
 
+        def open_side_by_side(name, k):
+            side_by_side[(name, k)] = grouped.tile([P, PASSES, P, PACK], BF16, tag="g" + name, name="g", align_bytes=64)
+
         def scale(name, source, k, g):
-            if g == 0:
-                side_by_side[(name, k)] = grouped.tile([P, PASSES, P, PACK], BF16, tag="g" + name, name="g", align_bytes=64)
             along = inverse[(name, k // GROUPS)][:].rearrange("p (c i) -> p c i", i=RUN)
             nc.vector.tensor_tensor(
                 out=side_by_side[(name, k)][:, g, :, :].rearrange("p (c i) t -> p c t i", i=RUN),
                 in0=source[:, g, :, :].rearrange("p t (c i) -> p c t i", i=RUN),
                 in1=along.unsqueeze(2).to_broadcast([P, P // RUN, PACK, RUN]),
+                op=ALU.mult,
+            )
+
+        def scale_on_gpsimd(name, source, k, g):
+            nc.gpsimd.tensor_tensor(
+                out=side_by_side[(name, k)][:, g, :, :],
+                in0=source[:, g, :, :].rearrange("p t c -> p c t"),
+                in1=inverse[(name, k // GROUPS)][:].unsqueeze(2).to_broadcast([P, P, PACK]),
                 op=ALU.mult,
             )
 
@@ -313,21 +322,23 @@ def tile_gmpahead_pb_k_kernel(tc, emb, gamma, beta, fc1d, out):
                 square("bn", bn_t[r - BN], r - BN)
 
             long_steps = []
-            k = r - SCALE_BN
-            if is_slot(k):
-                long_steps.extend([lambda g=g, k=k: scale("bn", bn_t[k], k, g) for g in range(PASSES)])
-            k = r - STATS
-            if is_slot(k):
-                long_steps.extend([lambda s=s, k=k: statistics(k, s) for s in range(PAIRS // 2)])
             k = r - SCALE_FC
             if is_slot(k):
-                long_steps.extend([lambda g=g, k=k: scale("fc", fc_rows[k], k, g) for g in range(PASSES)])
+                open_side_by_side("fc", k)
+                scale_on_gpsimd("fc", fc_rows[k], k, 1)
+            k = r - STATS
+            if is_slot(k):
+                long_steps.extend([lambda s=s, k=k: statistics(k, s) for s in range(PAIRS)])
+            k = r - SCALE_BN
+            if is_slot(k):
+                open_side_by_side("bn", k)
+                long_steps.extend([lambda g=g, k=k: scale("bn", bn_t[k], k, g) for g in range(PASSES)])
+            k = r - SCALE_FC
+            if is_slot(k):
+                long_steps.append(lambda k=k: scale("fc", fc_rows[k], k, 0))
             k = r - SCALE_BN
             if is_slot(k):
                 long_steps.append(lambda k=k: quantise("bn", bn_packed, k))
-            k = r - STATS
-            if is_slot(k):
-                long_steps.extend([lambda s=s, k=k: statistics(k, s) for s in range(PAIRS // 2, PAIRS)])
             k = r - SCALE_FC
             if is_slot(k):
                 long_steps.append(lambda k=k: quantise("fc", fc_packed, k))

@@ -66,7 +66,8 @@ def tile_gmpahead_pb_k_kernel(tc, emb, gamma, beta, fc1d, out):
         grouped = stack.enter_context(tc.tile_pool(name="grouped", bufs=1))
         bn_packed = stack.enter_context(tc.tile_pool(name="bn_packed", bufs=3))
         fc_packed = stack.enter_context(tc.tile_pool(name="fc_packed", bufs=MULTIPLY - SCALE_FC + 2))
-        psum_turned = stack.enter_context(tc.psum_pool(name="psum_turned", bufs=5))
+        psum_turned = stack.enter_context(tc.psum_pool(name="psum_turned", bufs=4))
+        psum_inverse = stack.enter_context(tc.psum_pool(name="psum_inverse", bufs=1))
         psum_bn = stack.enter_context(tc.psum_pool(name="psum_bn", bufs=1))
         psum_fc = stack.enter_context(tc.psum_pool(name="psum_fc", bufs=1))
         psum_mx = stack.enter_context(tc.psum_pool(name="psum_mx", bufs=1))
@@ -76,6 +77,7 @@ def tile_gmpahead_pb_k_kernel(tc, emb, gamma, beta, fc1d, out):
         bn_eps = const.tile([P, 1], F32)
         nc.vector.memset(bn_eps[:], BN_EPS)
         logits = const.tile([P, BINS, P], F32)
+        inverses = psum_inverse.tile([P, 4, P], F32)
 
         emb_rows = {}
         fc_rows = {}
@@ -87,6 +89,7 @@ def tile_gmpahead_pb_k_kernel(tc, emb, gamma, beta, fc1d, out):
         sums = {}
         norm = {}
         inverse = {}
+        inverse_in_sbuf = {}
         side_by_side = {}
         codes = {}
         scales = {}
@@ -219,22 +222,23 @@ def tile_gmpahead_pb_k_kernel(tc, emb, gamma, beta, fc1d, out):
             return [lambda: nc.vector.reciprocal(out=one, in_=one)]
 
         def lay_along(name, n):
-            along = psum_turned.tile([P, PAIRS, P], F32, tag="turned")
+            inverse[(name, n)] = inverses[:, {"bn": 0, "fc": 2}[name] + n % 2, :]
             nc.tensor.matmul(
-                along[:, 0, :],
+                inverse[(name, n)],
                 lhsT=norm[(name, n)][:, 0:1].to_broadcast([P, P]),
                 rhs=ident_f32[:],
                 start=True,
                 stop=True,
             )
-            inverse[(name, n)] = small.tile([P, P], F32, tag="inverse" + name, name="inverse")
-            nc.scalar.copy(out=inverse[(name, n)][:], in_=along[:, 0, :])
+            if name == "fc":
+                inverse_in_sbuf[n] = small.tile([P, P], F32, tag="inverse_in_sbuf", name="inverse_in_sbuf")
+                nc.scalar.copy(out=inverse_in_sbuf[n][:], in_=inverse[(name, n)])
 
         def open_side_by_side(name, k):
             side_by_side[(name, k)] = grouped.tile([P, PASSES, P, PACK], BF16, tag="g" + name, name="g", align_bytes=64)
 
         def scale(name, source, k, g):
-            along = inverse[(name, k // GROUPS)][:].rearrange("p (c i) -> p c i", i=RUN)
+            along = inverse[(name, k // GROUPS)].rearrange("p (c i) -> p c i", i=RUN)
             nc.vector.tensor_tensor(
                 out=side_by_side[(name, k)][:, g, :, :].rearrange("p (c i) t -> p c t i", i=RUN),
                 in0=source[:, g, :, :].rearrange("p t (c i) -> p c t i", i=RUN),
@@ -246,7 +250,7 @@ def tile_gmpahead_pb_k_kernel(tc, emb, gamma, beta, fc1d, out):
             nc.gpsimd.tensor_tensor(
                 out=side_by_side[(name, k)][:, g, :, :],
                 in0=source[:, g, :, :].rearrange("p t c -> p c t"),
-                in1=inverse[(name, k // GROUPS)][:].unsqueeze(2).to_broadcast([P, P, PACK]),
+                in1=inverse_in_sbuf[k // GROUPS][:].unsqueeze(2).to_broadcast([P, P, PACK]),
                 op=ALU.mult,
             )
 

@@ -50,6 +50,10 @@ def is_slot(k):
     return 0 <= k < SLOTS
 
 
+def squared_by_vector(k):
+    return BN <= k + FC_SQUARES < SCALE_BN and k % 2 == 1
+
+
 def bin_ended_by(k):
     return k // GROUPS if is_slot(k) and k % GROUPS == GROUPS - 1 else None
 
@@ -192,6 +196,11 @@ def tile_gmpahead_pb_k_kernel(tc, emb, gamma, beta, fc1d, out):
                 out=squares[(name, k)][:], in_=source[:].rearrange("p g t c -> p (g t) c"), func=ACT.Square
             )
 
+        def square_on_vector(name, source, k):
+            squares[(name, k)] = squares_pool.tile([P, CHUNKS, P], F32, tag=name + "_squares", name="squares")
+            chunks = source[:].rearrange("p g t c -> p (g t) c")
+            nc.vector.tensor_tensor(out=squares[(name, k)][:], in0=chunks, in1=chunks, op=ALU.mult)
+
         def add_squares(name, pool, k):
             n, i = divmod(k, GROUPS)
             if i == 0:
@@ -320,8 +329,9 @@ def tile_gmpahead_pb_k_kernel(tc, emb, gamma, beta, fc1d, out):
                 norm_root("bn", bn_root)
             if is_slot(r - BN):
                 batch_norm(r - BN)
-            if is_slot(r - FC_SQUARES):
-                square("fc", fc_rows[r - FC_SQUARES], r - FC_SQUARES)
+            k = r - FC_SQUARES
+            if is_slot(k) and not squared_by_vector(k):
+                square("fc", fc_rows[k], k)
             if is_slot(r - BN):
                 square("bn", bn_t[r - BN], r - BN)
 
@@ -333,6 +343,9 @@ def tile_gmpahead_pb_k_kernel(tc, emb, gamma, beta, fc1d, out):
             k = r - STATS
             if is_slot(k):
                 long_steps.extend([lambda s=s, k=k: statistics(k, s) for s in range(PAIRS)])
+            k = r - FC_SQUARES
+            if is_slot(k) and squared_by_vector(k):
+                long_steps.append(lambda k=k: square_on_vector("fc", fc_rows[k], k))
             k = r - SCALE_BN
             if is_slot(k):
                 open_side_by_side("bn", k)

@@ -23,7 +23,7 @@ PASSES = SLOT_FEATURES // (P * PACK)
 PAIRS = SLOT_FEATURES // (2 * P)
 CHUNKS = SLOT_FEATURES // P
 BIN_PAIRS = GROUPS * PAIRS
-RUN = 4
+RUN = 2
 BN_EPS = 1e-5
 L2_EPS = 1e-12
 

@@ -43,6 +43,7 @@ FC_SQUARES = 0
 ADD_FC_SQUARES = FC_SQUARES + 1
 FC_NORM = ADD_FC_SQUARES + 1
 SCALE_FC = ADD_FC_SQUARES + GROUPS + 3
+QUANTISE_FC = SCALE_FC + 1
 MULTIPLY = SCALE_BN + 1
 
 
@@ -67,7 +68,7 @@ def tile_gmpahead_pb_k_kernel(tc, emb, gamma, beta, fc1d, out):
         bn_pool = stack.enter_context(tc.tile_pool(name="bn", bufs=SCALE_BN - BN + 2))
         small = stack.enter_context(tc.tile_pool(name="small", bufs=2))
         squares_pool = stack.enter_context(tc.tile_pool(name="squares", bufs=2))
-        grouped = stack.enter_context(tc.tile_pool(name="grouped", bufs=1))
+        grouped = stack.enter_context(tc.tile_pool(name="grouped", bufs=2))
         bn_packed = stack.enter_context(tc.tile_pool(name="bn_packed", bufs=3))
         fc_packed = stack.enter_context(tc.tile_pool(name="fc_packed", bufs=MULTIPLY - SCALE_FC + 2))
         psum_turned = stack.enter_context(tc.psum_pool(name="psum_turned", bufs=4))
@@ -93,7 +94,6 @@ def tile_gmpahead_pb_k_kernel(tc, emb, gamma, beta, fc1d, out):
         sums = {}
         norm = {}
         inverse = {}
-        inverse_in_sbuf = {}
         side_by_side = {}
         codes = {}
         scales = {}
@@ -231,17 +231,20 @@ def tile_gmpahead_pb_k_kernel(tc, emb, gamma, beta, fc1d, out):
             return [lambda: nc.vector.reciprocal(out=one, in_=one)]
 
         def lay_along(name, n):
-            inverse[(name, n)] = inverses[:, {"bn": 0, "fc": 2}[name] + n % 2, :]
+            along = inverses[:, n % 2 if name == "bn" else 2, :]
             nc.tensor.matmul(
-                inverse[(name, n)],
+                along,
                 lhsT=norm[(name, n)][:, 0:1].to_broadcast([P, P]),
                 rhs=ident_f32[:],
                 start=True,
                 stop=True,
             )
             if name == "fc":
-                inverse_in_sbuf[n] = small.tile([P, P], F32, tag="inverse_in_sbuf", name="inverse_in_sbuf")
-                nc.scalar.copy(out=inverse_in_sbuf[n][:], in_=inverse[(name, n)])
+                in_sbuf = small.tile([P, P], F32, tag="inverse_in_sbuf", name="inverse_in_sbuf")
+                nc.scalar.copy(out=in_sbuf[:], in_=along)
+                inverse[(name, n)] = in_sbuf[:]
+            else:
+                inverse[(name, n)] = along
 
         def open_side_by_side(name, k):
             side_by_side[(name, k)] = grouped.tile([P, PASSES, P, PACK], BF16, tag="g" + name, name="g", align_bytes=64)
@@ -256,12 +259,14 @@ def tile_gmpahead_pb_k_kernel(tc, emb, gamma, beta, fc1d, out):
             )
 
         def scale_on_gpsimd(name, source, k, g):
-            nc.gpsimd.tensor_tensor(
-                out=side_by_side[(name, k)][:, g, :, :],
-                in0=source[:, g, :, :].rearrange("p t c -> p c t"),
-                in1=inverse_in_sbuf[k // GROUPS][:].unsqueeze(2).to_broadcast([P, P, PACK]),
-                op=ALU.mult,
-            )
+            for half in range(2):
+                some = slice(P // 2 * half, P // 2 * (half + 1))
+                nc.gpsimd.tensor_tensor(
+                    out=side_by_side[(name, k)][:, g, some, :],
+                    in0=source[:, g, :, some].rearrange("p t c -> p c t"),
+                    in1=inverse[(name, k // GROUPS)][:, some].unsqueeze(2).to_broadcast([P, P // 2, PACK]),
+                    op=ALU.mult,
+                )
 
         def quantise(name, pool, k):
             codes[(name, k)] = pool.tile([P, PASSES * P], U32, tag="c" + name, name="c", align_bytes=64)
@@ -339,26 +344,28 @@ def tile_gmpahead_pb_k_kernel(tc, emb, gamma, beta, fc1d, out):
             k = r - SCALE_FC
             if is_slot(k):
                 open_side_by_side("fc", k)
-                scale_on_gpsimd("fc", fc_rows[k], k, 1)
+                for g in range(PASSES):
+                    if g == 1 or SCALE_BN <= r < STATS + SLOTS:
+                        scale_on_gpsimd("fc", fc_rows[k], k, g)
             k = r - STATS
             if is_slot(k):
                 long_steps.extend([lambda s=s, k=k: statistics(k, s) for s in range(PAIRS)])
             k = r - FC_SQUARES
             if is_slot(k) and squared_by_vector(k):
                 long_steps.append(lambda k=k: square_on_vector("fc", fc_rows[k], k))
+            k = r - SCALE_FC
+            if is_slot(k) and not SCALE_BN <= r < STATS + SLOTS:
+                long_steps.append(lambda k=k: scale("fc", fc_rows[k], k, 0))
             k = r - SCALE_BN
             if is_slot(k):
                 open_side_by_side("bn", k)
                 long_steps.extend([lambda g=g, k=k: scale("bn", bn_t[k], k, g) for g in range(PASSES)])
-            k = r - SCALE_FC
+            k = r - QUANTISE_FC
             if is_slot(k):
-                long_steps.append(lambda k=k: scale("fc", fc_rows[k], k, 0))
+                long_steps.append(lambda k=k: quantise("fc", fc_packed, k))
             k = r - SCALE_BN
             if is_slot(k):
                 long_steps.append(lambda k=k: quantise("bn", bn_packed, k))
-            k = r - SCALE_FC
-            if is_slot(k):
-                long_steps.append(lambda k=k: quantise("fc", fc_packed, k))
 
             short_steps = []
             if gain_bin is not None:

@@ -23,6 +23,8 @@ PASSES = SLOT_FEATURES // (P * PACK)
 PAIRS = SLOT_FEATURES // (2 * P)
 CHUNKS = SLOT_FEATURES // P
 BIN_PAIRS = GROUPS * PAIRS
+WHOLE = slice(0, P)
+HALVES = (slice(0, P // 2), slice(P // 2, P))
 RUN = 2
 BN_EPS = 1e-5
 L2_EPS = 1e-12
@@ -43,7 +45,6 @@ FC_SQUARES = 0
 ADD_FC_SQUARES = FC_SQUARES + 1
 FC_NORM = ADD_FC_SQUARES + 1
 SCALE_FC = ADD_FC_SQUARES + GROUPS + 3
-QUANTISE_FC = SCALE_FC + 1
 MULTIPLY = SCALE_BN + 1
 
 
@@ -68,7 +69,8 @@ def tile_gmpahead_pb_k_kernel(tc, emb, gamma, beta, fc1d, out):
         bn_pool = stack.enter_context(tc.tile_pool(name="bn", bufs=SCALE_BN - BN + 2))
         small = stack.enter_context(tc.tile_pool(name="small", bufs=2))
         squares_pool = stack.enter_context(tc.tile_pool(name="squares", bufs=2))
-        grouped = stack.enter_context(tc.tile_pool(name="grouped", bufs=2))
+        bn_grouped = stack.enter_context(tc.tile_pool(name="bn_grouped", bufs=2))
+        fc_grouped = stack.enter_context(tc.tile_pool(name="fc_grouped", bufs=1))
         bn_packed = stack.enter_context(tc.tile_pool(name="bn_packed", bufs=3))
         fc_packed = stack.enter_context(tc.tile_pool(name="fc_packed", bufs=MULTIPLY - SCALE_FC + 2))
         psum_turned = stack.enter_context(tc.psum_pool(name="psum_turned", bufs=4))
@@ -94,6 +96,7 @@ def tile_gmpahead_pb_k_kernel(tc, emb, gamma, beta, fc1d, out):
         sums = {}
         norm = {}
         inverse = {}
+        inverse_in_sbuf = {}
         side_by_side = {}
         codes = {}
         scales = {}
@@ -231,42 +234,37 @@ def tile_gmpahead_pb_k_kernel(tc, emb, gamma, beta, fc1d, out):
             return [lambda: nc.vector.reciprocal(out=one, in_=one)]
 
         def lay_along(name, n):
-            along = inverses[:, n % 2 if name == "bn" else 2, :]
+            inverse[(name, n)] = inverses[:, {"bn": 0, "fc": 2}[name] + n % 2, :]
             nc.tensor.matmul(
-                along,
+                inverse[(name, n)],
                 lhsT=norm[(name, n)][:, 0:1].to_broadcast([P, P]),
                 rhs=ident_f32[:],
                 start=True,
                 stop=True,
             )
-            if name == "fc":
-                in_sbuf = small.tile([P, P], F32, tag="inverse_in_sbuf", name="inverse_in_sbuf")
-                nc.scalar.copy(out=in_sbuf[:], in_=along)
-                inverse[(name, n)] = in_sbuf[:]
-            else:
-                inverse[(name, n)] = along
+            if name == "fc" or n == BINS - 1:
+                inverse_in_sbuf[(name, n)] = small.tile([P, P], F32, tag="inverse_in_sbuf" + name, name="inverse_in_sbuf")
+                nc.scalar.copy(out=inverse_in_sbuf[(name, n)][:], in_=inverse[(name, n)])
 
-        def open_side_by_side(name, k):
-            side_by_side[(name, k)] = grouped.tile([P, PASSES, P, PACK], BF16, tag="g" + name, name="g", align_bytes=64)
+        def open_side_by_side(name, pool, k):
+            side_by_side[(name, k)] = pool.tile([P, PASSES, P, PACK], BF16, tag="g" + name, name="g", align_bytes=64)
 
-        def scale(name, source, k, g):
-            along = inverse[(name, k // GROUPS)].rearrange("p (c i) -> p c i", i=RUN)
+        def scale(name, source, k, g, some):
+            along = inverse[(name, k // GROUPS)][:, some].rearrange("p (c i) -> p c i", i=RUN)
             nc.vector.tensor_tensor(
-                out=side_by_side[(name, k)][:, g, :, :].rearrange("p (c i) t -> p c t i", i=RUN),
-                in0=source[:, g, :, :].rearrange("p t (c i) -> p c t i", i=RUN),
-                in1=along.unsqueeze(2).to_broadcast([P, P // RUN, PACK, RUN]),
+                out=side_by_side[(name, k)][:, g, some, :].rearrange("p (c i) t -> p c t i", i=RUN),
+                in0=source[:, g, :, some].rearrange("p t (c i) -> p c t i", i=RUN),
+                in1=along.unsqueeze(2).to_broadcast([P, (some.stop - some.start) // RUN, PACK, RUN]),
                 op=ALU.mult,
             )
 
-        def scale_on_gpsimd(name, source, k, g):
-            for half in range(2):
-                some = slice(P // 2 * half, P // 2 * (half + 1))
-                nc.gpsimd.tensor_tensor(
-                    out=side_by_side[(name, k)][:, g, some, :],
-                    in0=source[:, g, :, some].rearrange("p t c -> p c t"),
-                    in1=inverse[(name, k // GROUPS)][:, some].unsqueeze(2).to_broadcast([P, P // 2, PACK]),
-                    op=ALU.mult,
-                )
+        def scale_on_gpsimd(name, source, k, g, some):
+            nc.gpsimd.tensor_tensor(
+                out=side_by_side[(name, k)][:, g, some, :],
+                in0=source[:, g, :, some].rearrange("p t c -> p c t"),
+                in1=inverse_in_sbuf[(name, k // GROUPS)][:, some].unsqueeze(2).to_broadcast([P, some.stop - some.start, PACK]),
+                op=ALU.mult,
+            )
 
         def quantise(name, pool, k):
             codes[(name, k)] = pool.tile([P, PASSES * P], U32, tag="c" + name, name="c", align_bytes=64)
@@ -340,13 +338,15 @@ def tile_gmpahead_pb_k_kernel(tc, emb, gamma, beta, fc1d, out):
             if is_slot(r - BN):
                 square("bn", bn_t[r - BN], r - BN)
 
+            both = SCALE_BN <= r < STATS + SLOTS
             long_steps = []
             k = r - SCALE_FC
             if is_slot(k):
-                open_side_by_side("fc", k)
-                for g in range(PASSES):
-                    if g == 1 or SCALE_BN <= r < STATS + SLOTS:
-                        scale_on_gpsimd("fc", fc_rows[k], k, g)
+                open_side_by_side("fc", fc_grouped, k)
+                if both:
+                    scale_on_gpsimd("fc", fc_rows[k], k, 0, HALVES[1])
+                for half in HALVES:
+                    scale_on_gpsimd("fc", fc_rows[k], k, 1, half)
             k = r - STATS
             if is_slot(k):
                 long_steps.extend([lambda s=s, k=k: statistics(k, s) for s in range(PAIRS)])
@@ -354,13 +354,19 @@ def tile_gmpahead_pb_k_kernel(tc, emb, gamma, beta, fc1d, out):
             if is_slot(k) and squared_by_vector(k):
                 long_steps.append(lambda k=k: square_on_vector("fc", fc_rows[k], k))
             k = r - SCALE_FC
-            if is_slot(k) and not SCALE_BN <= r < STATS + SLOTS:
-                long_steps.append(lambda k=k: scale("fc", fc_rows[k], k, 0))
+            if is_slot(k):
+                own = HALVES[0] if both else WHOLE
+                long_steps.append(lambda k=k, own=own: scale("fc", fc_rows[k], k, 0, own))
             k = r - SCALE_BN
             if is_slot(k):
-                open_side_by_side("bn", k)
-                long_steps.extend([lambda g=g, k=k: scale("bn", bn_t[k], k, g) for g in range(PASSES)])
-            k = r - QUANTISE_FC
+                open_side_by_side("bn", bn_grouped, k)
+                last_bin = k // GROUPS == BINS - 1
+                if last_bin:
+                    scale_on_gpsimd("bn", bn_t[k], k, 1, HALVES[1])
+                long_steps.append(lambda k=k: scale("bn", bn_t[k], k, 0, WHOLE))
+                own = HALVES[0] if last_bin else WHOLE
+                long_steps.append(lambda k=k, own=own: scale("bn", bn_t[k], k, 1, own))
+            k = r - SCALE_FC
             if is_slot(k):
                 long_steps.append(lambda k=k: quantise("fc", fc_packed, k))
             k = r - SCALE_BN

from contextlib import ExitStack

import concourse.mybir as mybir
from concourse.masks import make_identity

F32 = mybir.dt.float32
BF16 = mybir.dt.bfloat16
I32 = mybir.dt.int32
U32 = mybir.dt.uint32
U8 = mybir.dt.uint8
FP8X4 = mybir.dt.float8_e4m3fn_x4
ACT = mybir.ActivationFunctionType
ALU = mybir.AluOpType

P = 128
BINS = 7
FEATURES = 8192
PACK = 4
GROUPS = 8
SLOTS = BINS * GROUPS
SLOT_FEATURES = FEATURES // GROUPS
PASSES = SLOT_FEATURES // (P * PACK)
PAIRS = SLOT_FEATURES // (2 * P)
CHUNKS = SLOT_FEATURES // P
BIN_PAIRS = GROUPS * PAIRS
WHOLE = slice(0, P)
HALVES = (slice(0, P // 2), slice(P // 2, P))
RUN = 2
BN_EPS = 1e-5
L2_EPS = 1e-12

FLOPS = 2 * BINS * P * FEATURES * P

LOAD_EMB = -8
LOAD_FC = -7
TURN_FOR_STATS = -1
STATS = 0
GAIN = STATS + 1
TURN_FOR_BN = STATS + GROUPS
BN = TURN_FOR_BN + 1
ADD_BN_SQUARES = BN + 1
BN_NORM = ADD_BN_SQUARES + 1
SCALE_BN = ADD_BN_SQUARES + GROUPS + 3
FC_SQUARES = 0
ADD_FC_SQUARES = FC_SQUARES + 1
FC_NORM = ADD_FC_SQUARES + 1
SCALE_FC = ADD_FC_SQUARES + GROUPS + 3
MULTIPLY = SCALE_BN + 1


def is_slot(k):
    return 0 <= k < SLOTS


def squared_by_vector(k):
    return BN <= k + FC_SQUARES < SCALE_BN and k % 2 == 1


def bin_ended_by(k):
    return k // GROUPS if is_slot(k) and k % GROUPS == GROUPS - 1 else None


def tile_gmpahead_pb_k_kernel(tc, emb, gamma, beta, fc1d, out):
    nc = tc.nc
    with ExitStack() as stack:
        const = stack.enter_context(tc.tile_pool(name="const", bufs=1))
        emb_pool = stack.enter_context(tc.tile_pool(name="emb", bufs=TURN_FOR_BN - LOAD_EMB + 1))
        fc_pool = stack.enter_context(tc.tile_pool(name="fc", bufs=SCALE_FC - LOAD_FC + 1))
        bn_pool = stack.enter_context(tc.tile_pool(name="bn", bufs=SCALE_BN - BN + 2))
        small = stack.enter_context(tc.tile_pool(name="small", bufs=2))
        squares_pool = stack.enter_context(tc.tile_pool(name="squares", bufs=2))
        bn_grouped = stack.enter_context(tc.tile_pool(name="bn_grouped", bufs=2))
        fc_grouped = stack.enter_context(tc.tile_pool(name="fc_grouped", bufs=1))
        bn_packed = stack.enter_context(tc.tile_pool(name="bn_packed", bufs=3))
        fc_packed = stack.enter_context(tc.tile_pool(name="fc_packed", bufs=MULTIPLY - SCALE_FC + 2))
        psum_turned = stack.enter_context(tc.psum_pool(name="psum_turned", bufs=4))
        psum_inverse = stack.enter_context(tc.psum_pool(name="psum_inverse", bufs=1))
        psum_bn = stack.enter_context(tc.psum_pool(name="psum_bn", bufs=1))
        psum_fc = stack.enter_context(tc.psum_pool(name="psum_fc", bufs=1))
        psum_mx = stack.enter_context(tc.psum_pool(name="psum_mx", bufs=1))

        ident_f32 = const.tile([P, P], F32)
        make_identity(nc, ident_f32[:])
        bn_eps = const.tile([P, 1], F32)
        nc.vector.memset(bn_eps[:], BN_EPS)
        logits = const.tile([P, BINS, P], F32)
        inverses = psum_inverse.tile([P, 4, P], F32)

        emb_rows = {}
        fc_rows = {}
        for_stats = {}
        for_bn = {}
        bn_t = {}
        per_bin = {}
        squares = {}
        sums = {}
        norm = {}
        inverse = {}
        inverse_in_sbuf = {}
        side_by_side = {}
        codes = {}
        scales = {}
        acc = {}

        def load_emb(k):
            n, i = divmod(k, GROUPS)
            emb_rows[k] = emb_pool.tile([P, SLOT_FEATURES], BF16, tag="emb_rows", name="emb_rows")
            nc.sync.dma_start(out=emb_rows[k][:], in_=emb[n][:, SLOT_FEATURES * i : SLOT_FEATURES * (i + 1)])

        def load_fc(k):
            n, i = divmod(k, GROUPS)
            fc_rows[k] = fc_pool.tile([P, PASSES, PACK, P], BF16, tag="fc_rows", name="fc_rows")
            nc.sync.dma_start(
                out=fc_rows[k][:].rearrange("p g (u e) k -> p (g u) (e k)", e=2),
                in_=fc1d[n][SLOT_FEATURES * i : SLOT_FEATURES * (i + 1), :].rearrange("(c p e) k -> p c (e k)", p=P, e=2),
            )

        def turn(k):
            turned = psum_turned.tile([P, PAIRS, P], F32, tag="turned", name="turned")
            words = emb_rows[k][:].bitcast(F32)
            for s in range(PAIRS):
                nc.tensor.transpose(turned[:, s, :], words[:, P * s : P * (s + 1)], ident_f32[:])
            return turned

        affine_rows = const.tile([P, BINS, 2 * P], BF16)
        nc.vector.memset(affine_rows[64:128, :, :].bitcast(I32), 0)
        nc.scalar.dma_start(out=affine_rows[0:32, :, :], in_=gamma.rearrange("n (c x) -> c n x", x=2 * P))
        nc.scalar.dma_start(out=affine_rows[32:64, :, :], in_=beta.rearrange("n (c x) -> c n x", x=2 * P))
        affine = const.tile([P, BINS, 2 * BIN_PAIRS, 2], F32)

        def turn_affine():
            for first in range(0, BINS, PAIRS):
                count = min(PAIRS, BINS - first)
                flipped = psum_turned.tile([P, PAIRS, P], F32, tag="turned")
                for s in range(count):
                    nc.tensor.transpose(flipped[:, s, :], affine_rows[:, first + s, :].bitcast(F32), ident_f32[:])
                pairs = flipped[:].bitcast(BF16).rearrange("p s (r e) -> p s r e", e=2)
                nc.vector.tensor_copy(
                    out=affine[:, first : first + count, :, :], in_=pairs[:, 0:count, 0 : 2 * BIN_PAIRS, :]
                )

        def open_bin(n):
            per_bin[n] = {
                "stats": small.tile([P, BIN_PAIRS, 6], F32, tag="stats", name="stats"),
                "narrow": small.tile([P, BIN_PAIRS, 2], F32, tag="narrow", name="narrow"),
                "gain": small.tile([P, BIN_PAIRS, 2], F32, tag="gain", name="gain"),
                "shift": small.tile([P, BIN_PAIRS, 2], F32, tag="shift", name="shift"),
            }

        def statistics(k, s):
            n, i = divmod(k, GROUPS)
            both = for_stats[k][:].bitcast(BF16)
            nc.vector.bn_stats(out=per_bin[n]["stats"][:, PAIRS * i + s, :], in_=both[:, s, :])

        def deviation(n):
            moments = per_bin[n]["stats"][:].rearrange("p c (e m) -> p c e m", m=3)
            nc.scalar.activation(
                out=per_bin[n]["narrow"][:],
                in_=moments[:, :, :, 2],
                func=ACT.Sqrt,
                bias=bn_eps[:],
                scale=1.0 / P,
            )

        def gain_and_shift(n):
            moments = per_bin[n]["stats"][:].rearrange("p c (e m) -> p c e m", m=3)
            narrow = per_bin[n]["narrow"][:]
            gain = per_bin[n]["gain"][:]
            shift = per_bin[n]["shift"][:]
            gammas = affine[:, n, 0:BIN_PAIRS, :]
            betas = affine[:, n, BIN_PAIRS : 2 * BIN_PAIRS, :]
            mult = ALU.mult
            return [
                lambda: nc.vector.tensor_tensor(out=shift, in0=gammas, in1=moments[:, :, :, 1], op=mult),
                lambda: nc.vector.reciprocal(out=narrow, in_=narrow),
                lambda: nc.vector.tensor_tensor(out=gain, in0=gammas, in1=narrow, op=mult),
                lambda: nc.vector.tensor_tensor(out=shift, in0=shift, in1=narrow, op=mult),
                lambda: nc.vector.tensor_tensor(out=shift, in0=betas, in1=shift, op=ALU.subtract),
            ]

        def batch_norm(k):
            n, i = divmod(k, GROUPS)
            split = for_bn[k][:].bitcast(BF16).rearrange("p s (b e) -> p s b e", e=2)
            bn_t[k] = bn_pool.tile([P, PASSES, PACK, P], F32, tag="bn_t", name="bn_t")
            chunks = bn_t[k][:].rearrange("p g (u e) b -> p (g u) e b", e=2)
            for s in range(PAIRS):
                for e in range(2):
                    nc.scalar.activation(
                        out=chunks[:, s, e, :],
                        in_=split[:, s, :, e],
                        func=ACT.Identity,
                        bias=per_bin[n]["shift"][:, PAIRS * i + s, e : e + 1],
                        scale=per_bin[n]["gain"][:, PAIRS * i + s, e : e + 1],
                    )

        def square(name, source, k):
            squares[(name, k)] = squares_pool.tile([P, CHUNKS, P], F32, tag=name + "_squares", name="squares")
            nc.scalar.activation(
                out=squares[(name, k)][:], in_=source[:].rearrange("p g t c -> p (g t) c"), func=ACT.Square
            )

        def square_on_vector(name, source, k):
            squares[(name, k)] = squares_pool.tile([P, CHUNKS, P], F32, tag=name + "_squares", name="squares")
            chunks = source[:].rearrange("p g t c -> p (g t) c")
            nc.vector.tensor_tensor(out=squares[(name, k)][:], in0=chunks, in1=chunks, op=ALU.mult)

        def add_squares(name, pool, k):
            n, i = divmod(k, GROUPS)
            if i == 0:
                sums[(name, n)] = pool.tile([P, PAIRS, P], F32, tag="sums_" + name, name="sums")
            for q in range(CHUNKS):
                nc.tensor.matmul(
                    sums[(name, n)][:, 0, :],
                    lhsT=squares[(name, k)][:, q, :],
                    rhs=ident_f32[:],
                    is_transpose=True,
                    start=(i == 0 and q == 0),
                    stop=(i == GROUPS - 1 and q == CHUNKS - 1),
                )

        def sum_of_squares(name, n):
            norm[(name, n)] = small.tile([P, 1], F32, tag="norm" + name, name="norm")
            one = norm[(name, n)][:]
            return [
                lambda: nc.vector.reduce_sum(out=one, in_=sums[(name, n)][:, 0, :], axis=mybir.AxisListType.X),
                lambda: nc.vector.tensor_scalar_max(out=one, in0=one, scalar1=L2_EPS * L2_EPS),
            ]

        def norm_root(name, n):
            nc.scalar.activation(out=norm[(name, n)][:], in_=norm[(name, n)][:], func=ACT.Sqrt)

        def inverse_norm(name, n):
            one = norm[(name, n)][:]
            return [lambda: nc.vector.reciprocal(out=one, in_=one)]

        def lay_along(name, n):
            inverse[(name, n)] = inverses[:, {"bn": 0, "fc": 2}[name] + n % 2, :]
            nc.tensor.matmul(
                inverse[(name, n)],
                lhsT=norm[(name, n)][:, 0:1].to_broadcast([P, P]),
                rhs=ident_f32[:],
                start=True,
                stop=True,
            )
            if name == "fc" or n == BINS - 1:
                inverse_in_sbuf[(name, n)] = small.tile([P, P], F32, tag="inverse_in_sbuf" + name, name="inverse_in_sbuf")
                nc.scalar.copy(out=inverse_in_sbuf[(name, n)][:], in_=inverse[(name, n)])

        def open_side_by_side(name, pool, k):
            side_by_side[(name, k)] = pool.tile([P, PASSES, P, PACK], BF16, tag="g" + name, name="g", align_bytes=64)

        def scale(name, source, k, g, some):
            along = inverse[(name, k // GROUPS)][:, some].rearrange("p (c i) -> p c i", i=RUN)
            nc.vector.tensor_tensor(
                out=side_by_side[(name, k)][:, g, some, :].rearrange("p (c i) t -> p c t i", i=RUN),
                in0=source[:, g, :, some].rearrange("p t (c i) -> p c t i", i=RUN),
                in1=along.unsqueeze(2).to_broadcast([P, (some.stop - some.start) // RUN, PACK, RUN]),
                op=ALU.mult,
            )

        def scale_on_gpsimd(name, source, k, g, some):
            nc.gpsimd.tensor_tensor(
                out=side_by_side[(name, k)][:, g, some, :],
                in0=source[:, g, :, some].rearrange("p t c -> p c t"),
                in1=inverse_in_sbuf[(name, k // GROUPS)][:, some].unsqueeze(2).to_broadcast([P, some.stop - some.start, PACK]),
                op=ALU.mult,
            )

        def quantise(name, pool, k):
            codes[(name, k)] = pool.tile([P, PASSES * P], U32, tag="c" + name, name="c", align_bytes=64)
            scales[(name, k)] = pool.tile([P, PASSES * P], U8, tag="s" + name, name="s", align_bytes=64)
            nc.vector.quantize_mx(
                out=codes[(name, k)][:].bitcast(FP8X4),
                scales=scales[(name, k)][:],
                in_=side_by_side[(name, k)][:].rearrange("p g c t -> p (g c t)"),
            )

        def multiply(k):
            n, i = divmod(k, GROUPS)
            if i == 0:
                acc[n] = psum_mx.tile([P, PAIRS, P], F32, tag="acc", name="acc")
            for g in range(PASSES):
                one = slice(P * g, P * (g + 1))
                nc.tensor.matmul_mx(
                    out=acc[n][:, 0, :],
                    lhsT=codes[("bn", k)][:, one].bitcast(FP8X4),
                    lhsT_scale=scales[("bn", k)][:, one],
                    rhs=codes[("fc", k)][:, one].bitcast(FP8X4),
                    rhs_scale=scales[("fc", k)][:, one],
                    start=(i == 0 and g == 0),
                    stop=(i == GROUPS - 1 and g == PASSES - 1),
                )
            if i == GROUPS - 1:
                nc.scalar.copy(out=logits[:, n, :], in_=acc[n][:, 0, :])
                nc.sync.dma_start(out=out[:, n, :], in_=logits[:, n, :])

        def one_round(r):
            if is_slot(r - LOAD_EMB):
                load_emb(r - LOAD_EMB)
            if is_slot(r - LOAD_FC):
                load_fc(r - LOAD_FC)

            fc_bin = bin_ended_by(r - FC_NORM - 2)
            if fc_bin is not None:
                lay_along("fc", fc_bin)
            bn_bin = bin_ended_by(r - BN_NORM - 2)
            if bn_bin is not None:
                lay_along("bn", bn_bin)
            k = r - TURN_FOR_STATS
            if is_slot(k):
                if k % GROUPS == 0:
                    open_bin(k // GROUPS)
                for_stats[k] = turn(k)
            k = r - TURN_FOR_BN
            if is_slot(k):
                for_bn[k] = turn(k)
            if is_slot(r - ADD_FC_SQUARES):
                add_squares("fc", psum_fc, r - ADD_FC_SQUARES)
            if is_slot(r - ADD_BN_SQUARES):
                add_squares("bn", psum_bn, r - ADD_BN_SQUARES)
            if is_slot(r - MULTIPLY):
                multiply(r - MULTIPLY)

            gain_bin = bin_ended_by(r - GAIN)
            if gain_bin is not None:
                deviation(gain_bin)
            fc_root = bin_ended_by(r - FC_NORM - 1)
            if fc_root is not None:
                norm_root("fc", fc_root)
            bn_root = bin_ended_by(r - BN_NORM - 1)
            if bn_root is not None:
                norm_root("bn", bn_root)
            if is_slot(r - BN):
                batch_norm(r - BN)
            k = r - FC_SQUARES
            if is_slot(k) and not squared_by_vector(k):
                square("fc", fc_rows[k], k)
            if is_slot(r - BN):
                square("bn", bn_t[r - BN], r - BN)

            both = SCALE_BN <= r < STATS + SLOTS
            long_steps = []
            k = r - SCALE_FC
            if is_slot(k):
                open_side_by_side("fc", fc_grouped, k)
                if both:
                    scale_on_gpsimd("fc", fc_rows[k], k, 0, HALVES[1])
                for half in HALVES:
                    scale_on_gpsimd("fc", fc_rows[k], k, 1, half)
            k = r - STATS
            if is_slot(k):
                long_steps.extend([lambda s=s, k=k: statistics(k, s) for s in range(PAIRS)])
            k = r - FC_SQUARES
            if is_slot(k) and squared_by_vector(k):
                long_steps.append(lambda k=k: square_on_vector("fc", fc_rows[k], k))
            k = r - SCALE_FC
            if is_slot(k):
                own = HALVES[0] if both else WHOLE
                long_steps.append(lambda k=k, own=own: scale("fc", fc_rows[k], k, 0, own))
            k = r - SCALE_BN
            if is_slot(k):
                open_side_by_side("bn", bn_grouped, k)
                last_bin = k // GROUPS == BINS - 1
                if last_bin:
                    scale_on_gpsimd("bn", bn_t[k], k, 1, HALVES[1])
                long_steps.append(lambda k=k: scale("bn", bn_t[k], k, 0, WHOLE))
                own = HALVES[0] if last_bin else WHOLE
                long_steps.append(lambda k=k, own=own: scale("bn", bn_t[k], k, 1, own))
            k = r - SCALE_FC
            if is_slot(k):
                long_steps.append(lambda k=k: quantise("fc", fc_packed, k))
            k = r - SCALE_BN
            if is_slot(k):
                long_steps.append(lambda k=k: quantise("bn", bn_packed, k))

            short_steps = []
            if gain_bin is not None:
                short_steps.extend(gain_and_shift(gain_bin))
            fc_bin = bin_ended_by(r - FC_NORM)
            if fc_bin is not None:
                short_steps.extend(sum_of_squares("fc", fc_bin))
            bn_bin = bin_ended_by(r - BN_NORM)
            if bn_bin is not None:
                short_steps.extend(sum_of_squares("bn", bn_bin))
            if fc_root is not None:
                short_steps.extend(inverse_norm("fc", fc_root))
            if bn_root is not None:
                short_steps.extend(inverse_norm("bn", bn_root))
            for place in range(max(len(long_steps), len(short_steps))):
                if place < len(long_steps):
                    long_steps[place]()
                if place < len(short_steps):
                    short_steps[place]()

        with tc.manual_schedule():
            for r in range(LOAD_EMB, STATS + TURN_FOR_STATS):
                one_round(r)
            turn_affine()
            for r in range(STATS + TURN_FOR_STATS, SLOTS + MULTIPLY):
                one_round(r)
